import numpy as np
import ml_dtypes


def mxq(x, axis, fmt="e4m3"):
    dtype, down = {"e4m3": (ml_dtypes.float8_e4m3fn, 7), "e5m2": (ml_dtypes.float8_e5m2, 14)}[fmt]
    v = np.moveaxis(np.asarray(x, np.float32).astype(ml_dtypes.bfloat16).astype(np.float64), axis, -1)
    blocks = v.reshape(v.shape[:-1] + (-1, 32))
    amax = np.abs(blocks).max(-1, keepdims=True)
    byte = np.maximum(np.where(amax > 0, np.frexp(amax)[1] - 1 + 127, 0) - down, 1)
    scale = np.exp2(byte - 127.0)
    codes = (blocks / scale).astype(np.float32).astype(dtype).astype(np.float64)
    return np.moveaxis((codes * scale).reshape(v.shape), -1, axis)


WIDE = False


def mx_kscale(k):
    if not WIDE:
        return np.ones(k)
    levels = np.array([10, -10, 5, -5, 0])
    a = np.random.permutation(np.resize(levels, k // 512 * 4)).reshape(k // 512, 4)
    idx = np.arange(k)
    return np.exp2(a[idx // 512, idx % 128 // 32])


BF16 = ml_dtypes.bfloat16


def bf(x):
    return np.asarray(x, np.float32).astype(BF16)


def f64(x):
    return np.asarray(x).astype(np.float64)


B, LQ, LS, D, SIM = 16, 256, 1024, 512, 1024
EPS = 1e-08


def l2norm(x):
    return x / (np.sqrt(np.sum(x * x, axis=-1, keepdims=True)) + EPS)


def setup_inputs():
    s = mx_kscale(D)
    return {"query": bf(np.random.standard_normal((B, LQ, D)) * 0.125 / s),
            "context": bf(np.random.standard_normal((B, LS, D)) * 2.0 * s),
            "matrix": bf(np.random.uniform(size=(B, LQ, D))),
            "smooth": 9}


def reference(query, context, matrix, smooth):
    c = f64(context)
    q = f64(query) * f64(matrix)
    attn = mxq(c, 2, "e4m3") @ mxq(q, 2, "e4m3").transpose(0, 2, 1)
    attn = np.where(attn >= 0, attn, 0.1 * attn)
    attn = l2norm(attn)
    z = attn.transpose(0, 2, 1) * smooth
    e = np.exp(z - z.max(-1, keepdims=True))
    p = e / e.sum(-1, keepdims=True)
    return mxq(p, 2, "e4m3") @ mxq(c, 1, "e4m3")

@@ -1,0 +1,225 @@
+from contextlib import ExitStack
+
+import concourse.mybir as mybir
+from concourse.masks import make_identity
+
+F32 = mybir.dt.float32
+BF16 = mybir.dt.bfloat16
+U32 = mybir.dt.uint32
+U8 = mybir.dt.uint8
+FP8X4 = mybir.dt.float8_e4m3fn_x4
+ALU = mybir.AluOpType
+ACT = mybir.ActivationFunctionType
+AX = mybir.AxisListType
+
+B, LQ, LS, D = 16, 256, 1024, 512
+P = 128
+EPS = 1e-08
+SLOPE = 0.1
+FLOPS = 2 * 2 * B * LQ * LS * D
+
+NT = LS // P
+NG = LS // 512
+NJ = LQ // P
+
+
+def tile_alignment_vector_pa_t_kernel(tc, query, context, matrix, smooth, out):
+    nc = tc.nc
+    smooth = float(smooth)
+    with ExitStack() as ctx:
+        consts = ctx.enter_context(tc.tile_pool(name="consts", bufs=1))
+        io = ctx.enter_context(tc.tile_pool(name="io", bufs=3))
+        work = ctx.enter_context(tc.tile_pool(name="work", bufs=2))
+        psum = ctx.enter_context(tc.psum_pool(name="psum", bufs=2))
+
+        ident_f = consts.tile([P, P], F32, name="ident_f")
+        make_identity(nc, ident_f[:])
+        ident_b = consts.tile([P, P], BF16, name="ident_b")
+        make_identity(nc, ident_b[:])
+        half = consts.tile([P, NT], F32, name="half")
+        nc.vector.memset(half[:], 0.5)
+
+        st = {}
+
+        def load(n):
+            c_sb = io.tile([P, NG, 4, D], BF16, name="c_sb")
+            nc.sync.dma_start(out=c_sb[:], in_=context[n].rearrange("(g p j) d -> p g j d", g=NG, p=P, j=4))
+            qr = io.tile([P, NJ, D], BF16, name="qr")
+            nc.sync.dma_start(out=qr[:], in_=query[n].rearrange("(p t) d -> p t d", t=NJ))
+            mt = io.tile([P, NJ, D], BF16, name="mt")
+            nc.sync.dma_start(out=mt[:], in_=matrix[n].rearrange("(p t) d -> p t d", t=NJ))
+            st[("c_sb", n)] = c_sb
+            st[("qr", n)] = qr
+            st[("mt", n)] = mt
+
+        def prep(n):
+            c_sb = st[("c_sb", n)]
+            qr = st[("qr", n)]
+            mt = st[("mt", n)]
+            q_sb = work.tile([P, NJ, D], BF16, name="q_sb")
+            nc.vector.tensor_tensor(out=q_sb[:], in0=qr[:], in1=mt[:], op=ALU.mult)
+            qT_ps = psum.tile([P, NJ, 4, P], BF16, name="qT_ps", bufs=1)
+            for jt in range(NJ):
+                qv = q_sb[:, jt, :].rearrange("p (u w e) -> p u e w", u=2, e=2)
+                for u in range(2):
+                    for e in range(2):
+                        nc.tensor.transpose(qT_ps[:, jt, 2 * u + e, :], qv[:, u, e, :], ident_b[:])
+            qg = work.tile([P, LQ, 4], BF16, name="qg", align_bytes=64)
+            nc.scalar.copy(
+                out=qg[:].rearrange("p (jt w) t -> p jt w t", jt=NJ),
+                in_=qT_ps[:].rearrange("p jt t w -> p jt w t"),
+            )
+            st[("qg", n)] = qg
+            c32 = c_sb[:].bitcast(F32)
+            cTg = work.tile([P, LS, 4], BF16, name="cTg", align_bytes=64)
+            cTg32 = cTg[:].bitcast(F32)
+            for b in range(NT // 2):
+                tr_ps = psum.tile([P, 2, 2, P], F32, name="tr_ps", bufs=2)
+                for i2 in range(2):
+                    i = 2 * b + i2
+                    for u in range(2):
+                        nc.tensor.transpose(tr_ps[:, i2, u, :], c32[:, i // 4, i % 4, P * u : P * (u + 1)], ident_f[:])
+                nc.scalar.copy(
+                    out=cTg32[:, 2 * P * b : 2 * P * (b + 1), :].rearrange("p (i s) u -> p i s u", i=2),
+                    in_=tr_ps[:].rearrange("p i u s -> p i s u"),
+                )
+            st[("cTg", n)] = cTg
+            cg = work.tile([P, NG, D, 4], BF16, name="cg", align_bytes=64)
+            for g in range(NG):
+                nc.vector.tensor_copy(
+                    out=cg[:, g].rearrange("p (c i) t -> p c t i", i=4),
+                    in_=c_sb[:, g].rearrange("p t (c i) -> p c t i", i=4),
+                )
+            st[("cg", n)] = cg
+
+        def quant(n):
+            qg = st[("qg", n)]
+            cTg = st[("cTg", n)]
+            cg = st[("cg", n)]
+            q_codes = work.tile([P, LQ], U32, name="q_codes", align_bytes=64)
+            q_scales = work.tile([P, LQ], U8, name="q_scales", align_bytes=64)
+            nc.vector.quantize_mx(out=q_codes[:].bitcast(FP8X4), scales=q_scales[:], in_=qg[:].rearrange("p j t -> p (j t)"))
+            cT_codes = work.tile([P, LS], U32, name="cT_codes", align_bytes=64)
+            cT_scales = work.tile([P, LS], U8, name="cT_scales", align_bytes=64)
+            nc.vector.quantize_mx(out=cT_codes[:].bitcast(FP8X4), scales=cT_scales[:], in_=cTg[:].rearrange("p s t -> p (s t)"))
+            c_codes = work.tile([P, NG * D], U32, name="c_codes", align_bytes=64, bufs=4)
+            c_scales = work.tile([P, NG * D], U8, name="c_scales", align_bytes=64, bufs=4)
+            nc.vector.quantize_mx(out=c_codes[:].bitcast(FP8X4), scales=c_scales[:], in_=cg[:].rearrange("p g d t -> p (g d t)"))
+            st[("q", n)] = (q_codes, q_scales)
+            st[("cT", n)] = (cT_codes, cT_scales)
+            st[("c", n)] = (c_codes, c_scales)
+
+        def score(n):
+            q_codes, q_scales = st[("q", n)]
+            cT_codes, cT_scales = st[("cT", n)]
+            lr = work.tile([P, NT, LQ], F32, name="lr", bufs=3)
+            ss = work.tile([P, NT], F32, name="ss")
+            for b in range(NT // 2):
+                a_ps = psum.tile([P, 2, LQ], F32, name="a_ps", bufs=2)
+                for i2 in range(2):
+                    i = 2 * b + i2
+                    nc.tensor.matmul_mx(
+                        out=a_ps[:, i2, :],
+                        lhsT=cT_codes[:, P * i : P * (i + 1)].bitcast(FP8X4),
+                        lhsT_scale=cT_scales[:, P * i : P * (i + 1)],
+                        rhs=q_codes[:].bitcast(FP8X4),
+                        rhs_scale=q_scales[:],
+                        start=True,
+                        stop=True,
+                    )
+                nc.scalar.mul(out=lr[:, 2 * b : 2 * b + 2, :], in_=a_ps[:], mul=SLOPE)
+                nc.vector.tensor_tensor(out=lr[:, 2 * b : 2 * b + 2, :], in0=a_ps[:], in1=lr[:, 2 * b : 2 * b + 2, :], op=ALU.max)
+                for i2 in range(2):
+                    i = 2 * b + i2
+                    junk = work.tile([P, LQ], BF16, name="junk")
+                    nc.scalar.activation(out=junk[:], in_=lr[:, i, :], func=ACT.Square, accum_out=ss[:, i : i + 1])
+            nrm = work.tile([P, NT], F32, name="nrm")
+            nc.gpsimd.tensor_tensor(out=nrm[:], in0=ss[:], in1=half[:], op=ALU.pow)
+            nre = work.tile([P, NT], F32, name="nre")
+            nc.vector.tensor_scalar(out=nre[:], in0=nrm[:], scalar1=EPS, scalar2=None, op0=ALU.add)
+            rec = work.tile([P, NT], F32, name="rec")
+            nc.vector.reciprocal(out=rec[:], in_=nre[:])
+            kk = work.tile([P, NT], F32, name="kk")
+            nc.vector.tensor_scalar(out=kk[:], in0=rec[:], scalar1=smooth, scalar2=None, op0=ALU.mult)
+            st[("lr", n)] = lr
+            st[("kk", n)] = kk
+
+        def expo(n):
+            lr = st[("lr", n)]
+            kk = st[("kk", n)]
+            ex = work.tile([P, NT, LQ], F32, name="ex")
+            for i in range(NT):
+                nc.scalar.activation(out=ex[:, i, :], in_=lr[:, i, :], func=ACT.Exp, scale=kk[:, i : i + 1], bias=-smooth)
+            es_ps = psum.tile([P, 4, P], F32, name="es_ps", bufs=1)
+            for jt in range(NJ):
+                for i in range(NT):
+                    nc.tensor.matmul(
+                        out=es_ps[:, jt, :],
+                        lhsT=ex[:, i, P * jt : P * (jt + 1)],
+                        rhs=ident_f[:],
+                        is_transpose=True,
+                        start=(i == 0),
+                        stop=(i == NT - 1),
+                    )
+            sm = work.tile([P, NJ], F32, name="sm")
+            nc.vector.tensor_reduce(out=sm[:], in_=es_ps[:, 0:NJ, :], axis=AX.X, op=ALU.add)
+            rs = work.tile([P, NJ], F32, name="rs")
+            nc.vector.reciprocal(out=rs[:], in_=sm[:])
+            for jt in range(NJ):
+                nc.tensor.matmul(
+                    out=es_ps[:, NJ + jt, :],
+                    lhsT=rs[:, jt : jt + 1].to_broadcast([P, P]),
+                    rhs=ident_f[:],
+                    start=True,
+                    stop=True,
+                )
+            st[("ex", n)] = ex
+            st[("es", n)] = es_ps
+
+        def final(n):
+            ex = st[("ex", n)]
+            es_ps = st[("es", n)]
+            c_codes, c_scales = st[("c", n)]
+            pg = work.tile([P, NG, LQ, 4], BF16, name="pg", align_bytes=64)
+            rb = es_ps[:, NJ : 2 * NJ, :].rearrange("p t w -> p (t w)").unsqueeze(2).to_broadcast([P, LQ, 4])
+            for g in range(NG):
+                nc.vector.tensor_tensor(
+                    out=pg[:, g],
+                    in0=ex[:, 4 * g : 4 * (g + 1), :].rearrange("p t j -> p j t"),
+                    in1=rb,
+                    op=ALU.mult,
+                )
+            p_codes = work.tile([P, NG * LQ], U32, name="p_codes", align_bytes=64)
+            p_scales = work.tile([P, NG * LQ], U8, name="p_scales", align_bytes=64)
+            nc.vector.quantize_mx(out=p_codes[:].bitcast(FP8X4), scales=p_scales[:], in_=pg[:].rearrange("p g j t -> p (g j t)"))
+            o_sb = io.tile([P, NJ, D], F32, name="o_sb")
+            for jt in range(NJ):
+                o_ps = psum.tile([P, D], F32, name="o_ps", bufs=2)
+                for g in range(NG):
+                    lo = LQ * g + P * jt
+                    nc.tensor.matmul_mx(
+                        out=o_ps[:],
+                        lhsT=p_codes[:, lo : lo + P].bitcast(FP8X4),
+                        lhsT_scale=p_scales[:, lo : lo + P],
+                        rhs=c_codes[:, D * g : D * (g + 1)].bitcast(FP8X4),
+                        rhs_scale=c_scales[:, D * g : D * (g + 1)],
+                        start=(g == 0),
+                        stop=(g == NG - 1),
+                    )
+                nc.scalar.copy(out=o_sb[:, jt, :], in_=o_ps[:])
+            nc.sync.dma_start(out=out[n].rearrange("(p t) d -> p t d", t=NJ), in_=o_sb[:])
+
+        load(0)
+        load(1)
+        for it in range(B + 3):
+            if 0 <= it - 3 < B:
+                final(it - 3)
+            if 0 <= it - 2 < B:
+                expo(it - 2)
+            if 0 <= it - 1 < B:
+                score(it - 1)
+            if it < B:
+                prep(it)
+                quant(it)
+            if it + 2 < B:
+                load(it + 2)

@@ -21,6 +21,40 @@ FLOPS = 2 * 2 * B * LQ * LS * D
 NT = LS // P
 NG = LS // 512
 NJ = LQ // P
+NQ = 4
+
+SCHEDULE = (
+    ("load", -12, 0),
+    ("mm1", -1, None),
+    ("mm2", 15, 0),
+    ("mm2", 15, 1),
+    ("ctr", -4, None),
+    ("qtr", -5, 0),
+    ("etr", 10, 0),
+    ("kk", 6, 0),
+    ("red", 11, 0),
+    ("cTq", -2, None),
+    ("cq", -3, None),
+    ("rb", 11, 0),
+    ("p0", 0, None),
+    ("p2", 1, None),
+    ("pw", 4, 0),
+    ("ex", 6, None),
+    ("cTe", -3, None),
+    ("qe", -4, 0),
+    ("qe", -3, 1),
+    ("oe", 15, 0),
+    ("oe", 16, 1),
+    ("store", 16, 0),
+    ("cg", -4, None),
+    ("p1", 0, None),
+    ("qq", -2, 0),
+    ("gate", -6, 0),
+    ("pj", 12, 0),
+    ("pj", 13, 1),
+    ("pq", 14, 0),
+    ("pq", 14, 1),
+)
 
 
 def tile_alignment_vector_pa_t_kernel(tc, query, context, matrix, smooth, out):
@@ -28,8 +62,7 @@ def tile_alignment_vector_pa_t_kernel(tc, query, context, matrix, smooth, out):
     smooth = float(smooth)
     with ExitStack() as ctx:
         consts = ctx.enter_context(tc.tile_pool(name="consts", bufs=1))
-        io = ctx.enter_context(tc.tile_pool(name="io", bufs=3))
-        work = ctx.enter_context(tc.tile_pool(name="work", bufs=2))
+        sb = ctx.enter_context(tc.tile_pool(name="sb", bufs=2))
         psum = ctx.enter_context(tc.psum_pool(name="psum", bufs=2))
 
         ident_f = consts.tile([P, P], F32, name="ident_f")
@@ -41,185 +74,256 @@ def tile_alignment_vector_pa_t_kernel(tc, query, context, matrix, smooth, out):
 
         st = {}
 
-        def load(n):
-            c_sb = io.tile([P, NG, 4, D], BF16, name="c_sb")
+        def load(n, arg):
+            c_sb = sb.tile([P, NG, 4, D], BF16, name="c_sb", bufs=3)
             nc.sync.dma_start(out=c_sb[:], in_=context[n].rearrange("(g p j) d -> p g j d", g=NG, p=P, j=4))
-            qr = io.tile([P, NJ, D], BF16, name="qr")
+            qr = sb.tile([P, NJ, D], BF16, name="qr", bufs=3)
             nc.sync.dma_start(out=qr[:], in_=query[n].rearrange("(p t) d -> p t d", t=NJ))
-            mt = io.tile([P, NJ, D], BF16, name="mt")
+            mt = sb.tile([P, NJ, D], BF16, name="mt", bufs=3)
             nc.sync.dma_start(out=mt[:], in_=matrix[n].rearrange("(p t) d -> p t d", t=NJ))
             st[("c_sb", n)] = c_sb
             st[("qr", n)] = qr
             st[("mt", n)] = mt
 
-        def prep(n):
-            c_sb = st[("c_sb", n)]
-            qr = st[("qr", n)]
-            mt = st[("mt", n)]
-            q_sb = work.tile([P, NJ, D], BF16, name="q_sb")
-            nc.vector.tensor_tensor(out=q_sb[:], in0=qr[:], in1=mt[:], op=ALU.mult)
+        def gate(n, arg):
+            q_sb = sb.tile([P, NJ, D], BF16, name="q_sb")
+            nc.vector.tensor_tensor(out=q_sb[:], in0=st[("qr", n)][:], in1=st[("mt", n)][:], op=ALU.mult)
+            st[("q_sb", n)] = q_sb
+
+        def qtr(n, arg):
+            q_sb = st[("q_sb", n)]
             qT_ps = psum.tile([P, NJ, 4, P], BF16, name="qT_ps", bufs=1)
             for jt in range(NJ):
                 qv = q_sb[:, jt, :].rearrange("p (u w e) -> p u e w", u=2, e=2)
                 for u in range(2):
                     for e in range(2):
                         nc.tensor.transpose(qT_ps[:, jt, 2 * u + e, :], qv[:, u, e, :], ident_b[:])
-            qg = work.tile([P, LQ, 4], BF16, name="qg", align_bytes=64)
+            st[("qT_ps", n)] = qT_ps
+            st[("qg", n)] = sb.tile([P, LQ, 4], BF16, name="qg", align_bytes=64)
+
+        def qe(n, jt):
             nc.scalar.copy(
-                out=qg[:].rearrange("p (jt w) t -> p jt w t", jt=NJ),
-                in_=qT_ps[:].rearrange("p jt t w -> p jt w t"),
+                out=st[("qg", n)][:, P * jt : P * (jt + 1), :],
+                in_=st[("qT_ps", n)][:, jt].rearrange("p t w -> p w t"),
             )
-            st[("qg", n)] = qg
-            c32 = c_sb[:].bitcast(F32)
-            cTg = work.tile([P, LS, 4], BF16, name="cTg", align_bytes=64)
-            cTg32 = cTg[:].bitcast(F32)
-            for b in range(NT // 2):
-                tr_ps = psum.tile([P, 2, 2, P], F32, name="tr_ps", bufs=2)
-                for i2 in range(2):
-                    i = 2 * b + i2
-                    for u in range(2):
-                        nc.tensor.transpose(tr_ps[:, i2, u, :], c32[:, i // 4, i % 4, P * u : P * (u + 1)], ident_f[:])
-                nc.scalar.copy(
-                    out=cTg32[:, 2 * P * b : 2 * P * (b + 1), :].rearrange("p (i s) u -> p i s u", i=2),
-                    in_=tr_ps[:].rearrange("p i u s -> p i s u"),
-                )
-            st[("cTg", n)] = cTg
-            cg = work.tile([P, NG, D, 4], BF16, name="cg", align_bytes=64)
-            for g in range(NG):
-                nc.vector.tensor_copy(
-                    out=cg[:, g].rearrange("p (c i) t -> p c t i", i=4),
-                    in_=c_sb[:, g].rearrange("p t (c i) -> p c t i", i=4),
-                )
-            st[("cg", n)] = cg
 
-        def quant(n):
-            qg = st[("qg", n)]
-            cTg = st[("cTg", n)]
-            cg = st[("cg", n)]
-            q_codes = work.tile([P, LQ], U32, name="q_codes", align_bytes=64)
-            q_scales = work.tile([P, LQ], U8, name="q_scales", align_bytes=64)
-            nc.vector.quantize_mx(out=q_codes[:].bitcast(FP8X4), scales=q_scales[:], in_=qg[:].rearrange("p j t -> p (j t)"))
-            cT_codes = work.tile([P, LS], U32, name="cT_codes", align_bytes=64)
-            cT_scales = work.tile([P, LS], U8, name="cT_scales", align_bytes=64)
-            nc.vector.quantize_mx(out=cT_codes[:].bitcast(FP8X4), scales=cT_scales[:], in_=cTg[:].rearrange("p s t -> p (s t)"))
-            c_codes = work.tile([P, NG * D], U32, name="c_codes", align_bytes=64, bufs=4)
-            c_scales = work.tile([P, NG * D], U8, name="c_scales", align_bytes=64, bufs=4)
-            nc.vector.quantize_mx(out=c_codes[:].bitcast(FP8X4), scales=c_scales[:], in_=cg[:].rearrange("p g d t -> p (g d t)"))
+        def qq(n, arg):
+            q_codes = sb.tile([P, LQ], U32, name="q_codes", align_bytes=64)
+            q_scales = sb.tile([P, LQ], U8, name="q_scales", align_bytes=64)
+            nc.vector.quantize_mx(
+                out=q_codes[:].bitcast(FP8X4), scales=q_scales[:], in_=st[("qg", n)][:].rearrange("p j t -> p (j t)")
+            )
             st[("q", n)] = (q_codes, q_scales)
-            st[("cT", n)] = (cT_codes, cT_scales)
-            st[("c", n)] = (c_codes, c_scales)
 
-        def score(n):
+        def ctr(n, b):
+            c32 = st[("c_sb", n)][:].bitcast(F32)
+            tr_ps = psum.tile([P, 2, 2, P], F32, name="tr_ps", bufs=2)
+            for i2 in range(2):
+                i = 2 * b + i2
+                for u in range(2):
+                    nc.tensor.transpose(tr_ps[:, i2, u, :], c32[:, i // 4, i % 4, P * u : P * (u + 1)], ident_f[:])
+            st[("tr_ps", n, b)] = tr_ps
+
+        def cTe(n, b):
+            if b == 0:
+                st[("cTg", n)] = sb.tile([P, LS, 4], BF16, name="cTg", align_bytes=64)
+            cTg32 = st[("cTg", n)][:].bitcast(F32)
+            nc.scalar.copy(
+                out=cTg32[:, 2 * P * b : 2 * P * (b + 1), :].rearrange("p (i s) u -> p i s u", i=2),
+                in_=st[("tr_ps", n, b)][:].rearrange("p i u s -> p i s u"),
+            )
+
+        def cTq(n, b):
+            if b == 0:
+                st[("cT", n)] = (
+                    sb.tile([P, LS], U32, name="cT_codes", align_bytes=64),
+                    sb.tile([P, LS], U8, name="cT_scales", align_bytes=64),
+                )
+            cT_codes, cT_scales = st[("cT", n)]
+            cols = slice(2 * P * b, 2 * P * (b + 1))
+            nc.vector.quantize_mx(
+                out=cT_codes[:, cols].bitcast(FP8X4),
+                scales=cT_scales[:, cols],
+                in_=st[("cTg", n)][:, cols, :].rearrange("p s t -> p (s t)"),
+            )
+
+        def cg(n, b):
+            if b == 0:
+                st[("cg", n)] = sb.tile([P, NG, D, 4], BF16, name="cg", align_bytes=64)
+            g, h = b // 2, b % 2
+            cols = slice(256 * h, 256 * (h + 1))
+            nc.vector.tensor_copy(
+                out=st[("cg", n)][:, g, cols, :].rearrange("p (c i) t -> p c t i", i=4),
+                in_=st[("c_sb", n)][:, g, :, cols].rearrange("p t (c i) -> p c t i", i=4),
+            )
+
+        def cq(n, b):
+            if b == 0:
+                st[("c", n)] = (
+                    sb.tile([P, NG * D], U32, name="c_codes", align_bytes=64, bufs=6),
+                    sb.tile([P, NG * D], U8, name="c_scales", align_bytes=64, bufs=6),
+                )
+            c_codes, c_scales = st[("c", n)]
+            g, h = b // 2, b % 2
+            nc.vector.quantize_mx(
+                out=c_codes[:, 256 * b : 256 * (b + 1)].bitcast(FP8X4),
+                scales=c_scales[:, 256 * b : 256 * (b + 1)],
+                in_=st[("cg", n)][:, g, 256 * h : 256 * (h + 1), :].rearrange("p d t -> p (d t)"),
+            )
+
+        def mm1(n, b):
             q_codes, q_scales = st[("q", n)]
             cT_codes, cT_scales = st[("cT", n)]
-            lr = work.tile([P, NT, LQ], F32, name="lr", bufs=3)
-            ss = work.tile([P, NT], F32, name="ss")
-            for b in range(NT // 2):
-                a_ps = psum.tile([P, 2, LQ], F32, name="a_ps", bufs=2)
-                for i2 in range(2):
-                    i = 2 * b + i2
-                    nc.tensor.matmul_mx(
-                        out=a_ps[:, i2, :],
-                        lhsT=cT_codes[:, P * i : P * (i + 1)].bitcast(FP8X4),
-                        lhsT_scale=cT_scales[:, P * i : P * (i + 1)],
-                        rhs=q_codes[:].bitcast(FP8X4),
-                        rhs_scale=q_scales[:],
-                        start=True,
-                        stop=True,
-                    )
-                nc.scalar.mul(out=lr[:, 2 * b : 2 * b + 2, :], in_=a_ps[:], mul=SLOPE)
-                nc.vector.tensor_tensor(out=lr[:, 2 * b : 2 * b + 2, :], in0=a_ps[:], in1=lr[:, 2 * b : 2 * b + 2, :], op=ALU.max)
-                for i2 in range(2):
-                    i = 2 * b + i2
-                    junk = work.tile([P, LQ], BF16, name="junk")
-                    nc.scalar.activation(out=junk[:], in_=lr[:, i, :], func=ACT.Square, accum_out=ss[:, i : i + 1])
-            nrm = work.tile([P, NT], F32, name="nrm")
-            nc.gpsimd.tensor_tensor(out=nrm[:], in0=ss[:], in1=half[:], op=ALU.pow)
-            nre = work.tile([P, NT], F32, name="nre")
-            nc.vector.tensor_scalar(out=nre[:], in0=nrm[:], scalar1=EPS, scalar2=None, op0=ALU.add)
-            rec = work.tile([P, NT], F32, name="rec")
-            nc.vector.reciprocal(out=rec[:], in_=nre[:])
-            kk = work.tile([P, NT], F32, name="kk")
-            nc.vector.tensor_scalar(out=kk[:], in0=rec[:], scalar1=smooth, scalar2=None, op0=ALU.mult)
-            st[("lr", n)] = lr
-            st[("kk", n)] = kk
+            a_ps = psum.tile([P, 2, LQ], F32, name="a_ps", bufs=2)
+            for i2 in range(2):
+                i = 2 * b + i2
+                nc.tensor.matmul_mx(
+                    out=a_ps[:, i2, :],
+                    lhsT=cT_codes[:, P * i : P * (i + 1)].bitcast(FP8X4),
+                    lhsT_scale=cT_scales[:, P * i : P * (i + 1)],
+                    rhs=q_codes[:].bitcast(FP8X4),
+                    rhs_scale=q_scales[:],
+                    start=True,
+                    stop=True,
+                )
+            st[("a_ps", n, b)] = a_ps
 
-        def expo(n):
-            lr = st[("lr", n)]
-            kk = st[("kk", n)]
-            ex = work.tile([P, NT, LQ], F32, name="ex")
-            for i in range(NT):
-                nc.scalar.activation(out=ex[:, i, :], in_=lr[:, i, :], func=ACT.Exp, scale=kk[:, i : i + 1], bias=-smooth)
+        def p0(n, b):
+            if b == 0:
+                st[("lr", n)] = sb.tile([P, NT, LQ], F32, name="lr", bufs=4)
+                st[("ss", n)] = sb.tile([P, NT], F32, name="ss", bufs=3)
+            nc.scalar.mul(out=st[("lr", n)][:, 2 * b : 2 * b + 2, :], in_=st[("a_ps", n, b)][:], mul=SLOPE)
+
+        def p1(n, b):
+            part = st[("lr", n)][:, 2 * b : 2 * b + 2, :]
+            nc.vector.tensor_tensor(out=part, in0=st[("a_ps", n, b)][:], in1=part, op=ALU.max)
+
+        def p2(n, b):
+            for i in (2 * b, 2 * b + 1):
+                junk = sb.tile([P, LQ], BF16, name="junk")
+                nc.scalar.activation(
+                    out=junk[:], in_=st[("lr", n)][:, i, :], func=ACT.Square, accum_out=st[("ss", n)][:, i : i + 1]
+                )
+
+        def pw(n, arg):
+            nrm = sb.tile([P, NT], F32, name="nrm", bufs=3)
+            nc.gpsimd.tensor_tensor(out=nrm[:], in0=st[("ss", n)][:], in1=half[:], op=ALU.pow)
+            st[("nrm", n)] = nrm
+
+        def kk(n, arg):
+            nre = sb.tile([P, NT], F32, name="nre", bufs=3)
+            nc.vector.tensor_scalar(out=nre[:], in0=st[("nrm", n)][:], scalar1=EPS, scalar2=None, op0=ALU.add)
+            rec = sb.tile([P, NT], F32, name="rec", bufs=3)
+            nc.vector.reciprocal(out=rec[:], in_=nre[:])
+            kt = sb.tile([P, NT], F32, name="kt", bufs=3)
+            nc.vector.tensor_scalar(out=kt[:], in0=rec[:], scalar1=smooth, scalar2=None, op0=ALU.mult)
+            st[("kt", n)] = kt
+
+        def ex(n, b):
+            if b == 0:
+                st[("ex", n)] = sb.tile([P, NT, LQ], F32, name="ex")
+            for i in (2 * b, 2 * b + 1):
+                nc.scalar.activation(
+                    out=st[("ex", n)][:, i, :],
+                    in_=st[("lr", n)][:, i, :],
+                    func=ACT.Exp,
+                    scale=st[("kt", n)][:, i : i + 1],
+                    bias=-smooth,
+                )
+
+        def etr(n, arg):
             es_ps = psum.tile([P, 4, P], F32, name="es_ps", bufs=1)
             for jt in range(NJ):
                 for i in range(NT):
                     nc.tensor.matmul(
                         out=es_ps[:, jt, :],
-                        lhsT=ex[:, i, P * jt : P * (jt + 1)],
+                        lhsT=st[("ex", n)][:, i, P * jt : P * (jt + 1)],
                         rhs=ident_f[:],
                         is_transpose=True,
                         start=(i == 0),
                         stop=(i == NT - 1),
                     )
-            sm = work.tile([P, NJ], F32, name="sm")
-            nc.vector.tensor_reduce(out=sm[:], in_=es_ps[:, 0:NJ, :], axis=AX.X, op=ALU.add)
-            rs = work.tile([P, NJ], F32, name="rs")
+            st[("es", n)] = es_ps
+
+        def red(n, arg):
+            sm = sb.tile([P, NJ], F32, name="sm", bufs=3)
+            nc.vector.tensor_reduce(out=sm[:], in_=st[("es", n)][:, 0:NJ, :], axis=AX.X, op=ALU.add)
+            rs = sb.tile([P, NJ], F32, name="rs", bufs=3)
             nc.vector.reciprocal(out=rs[:], in_=sm[:])
+            st[("rs", n)] = rs
+
+        def rb(n, arg):
             for jt in range(NJ):
                 nc.tensor.matmul(
-                    out=es_ps[:, NJ + jt, :],
-                    lhsT=rs[:, jt : jt + 1].to_broadcast([P, P]),
+                    out=st[("es", n)][:, NJ + jt, :],
+                    lhsT=st[("rs", n)][:, jt : jt + 1].to_broadcast([P, P]),
                     rhs=ident_f[:],
                     start=True,
                     stop=True,
                 )
-            st[("ex", n)] = ex
-            st[("es", n)] = es_ps
 
-        def final(n):
-            ex = st[("ex", n)]
-            es_ps = st[("es", n)]
-            c_codes, c_scales = st[("c", n)]
-            pg = work.tile([P, NG, LQ, 4], BF16, name="pg", align_bytes=64)
-            rb = es_ps[:, NJ : 2 * NJ, :].rearrange("p t w -> p (t w)").unsqueeze(2).to_broadcast([P, LQ, 4])
-            for g in range(NG):
-                nc.vector.tensor_tensor(
-                    out=pg[:, g],
-                    in0=ex[:, 4 * g : 4 * (g + 1), :].rearrange("p t j -> p j t"),
-                    in1=rb,
-                    op=ALU.mult,
+        def pj(n, g):
+            if g == 0:
+                st[("pg", n)] = sb.tile([P, NG, LQ, 4], BF16, name="pg", align_bytes=64)
+            rbv = st[("es", n)][:, NJ : 2 * NJ, :].rearrange("p t w -> p (t w)").unsqueeze(2).to_broadcast([P, LQ, 4])
+            nc.vector.tensor_tensor(
+                out=st[("pg", n)][:, g],
+                in0=st[("ex", n)][:, 4 * g : 4 * (g + 1), :].rearrange("p t j -> p j t"),
+                in1=rbv,
+                op=ALU.mult,
+            )
+
+        def pq(n, g):
+            if g == 0:
+                st[("p", n)] = (
+                    sb.tile([P, NG * LQ], U32, name="p_codes", align_bytes=64),
+                    sb.tile([P, NG * LQ], U8, name="p_scales", align_bytes=64),
                 )
-            p_codes = work.tile([P, NG * LQ], U32, name="p_codes", align_bytes=64)
-            p_scales = work.tile([P, NG * LQ], U8, name="p_scales", align_bytes=64)
-            nc.vector.quantize_mx(out=p_codes[:].bitcast(FP8X4), scales=p_scales[:], in_=pg[:].rearrange("p g j t -> p (g j t)"))
-            o_sb = io.tile([P, NJ, D], F32, name="o_sb")
-            for jt in range(NJ):
-                o_ps = psum.tile([P, D], F32, name="o_ps", bufs=2)
-                for g in range(NG):
-                    lo = LQ * g + P * jt
-                    nc.tensor.matmul_mx(
-                        out=o_ps[:],
-                        lhsT=p_codes[:, lo : lo + P].bitcast(FP8X4),
-                        lhsT_scale=p_scales[:, lo : lo + P],
-                        rhs=c_codes[:, D * g : D * (g + 1)].bitcast(FP8X4),
-                        rhs_scale=c_scales[:, D * g : D * (g + 1)],
-                        start=(g == 0),
-                        stop=(g == NG - 1),
-                    )
-                nc.scalar.copy(out=o_sb[:, jt, :], in_=o_ps[:])
-            nc.sync.dma_start(out=out[n].rearrange("(p t) d -> p t d", t=NJ), in_=o_sb[:])
+            p_codes, p_scales = st[("p", n)]
+            nc.vector.quantize_mx(
+                out=p_codes[:, LQ * g : LQ * (g + 1)].bitcast(FP8X4),
+                scales=p_scales[:, LQ * g : LQ * (g + 1)],
+                in_=st[("pg", n)][:, g].rearrange("p j t -> p (j t)"),
+            )
 
-        load(0)
-        load(1)
-        for it in range(B + 3):
-            if 0 <= it - 3 < B:
-                final(it - 3)
-            if 0 <= it - 2 < B:
-                expo(it - 2)
-            if 0 <= it - 1 < B:
-                score(it - 1)
-            if it < B:
-                prep(it)
-                quant(it)
-            if it + 2 < B:
-                load(it + 2)
+        def mm2(n, jt):
+            p_codes, p_scales = st[("p", n)]
+            c_codes, c_scales = st[("c", n)]
+            o_ps = psum.tile([P, D], F32, name="o_ps", bufs=2)
+            for g in range(NG):
+                lo = LQ * g + P * jt
+                nc.tensor.matmul_mx(
+                    out=o_ps[:],
+                    lhsT=p_codes[:, lo : lo + P].bitcast(FP8X4),
+                    lhsT_scale=p_scales[:, lo : lo + P],
+                    rhs=c_codes[:, D * g : D * (g + 1)].bitcast(FP8X4),
+                    rhs_scale=c_scales[:, D * g : D * (g + 1)],
+                    start=(g == 0),
+                    stop=(g == NG - 1),
+                )
+            st[("o_ps", n, jt)] = o_ps
+
+        def oe(n, jt):
+            if jt == 0:
+                st[("o_sb", n)] = sb.tile([P, NJ, D], F32, name="o_sb", bufs=3)
+            nc.scalar.copy(out=st[("o_sb", n)][:, jt, :], in_=st[("o_ps", n, jt)][:])
+
+        def store(n, arg):
+            nc.sync.dma_start(out=out[n].rearrange("(p t) d -> p t d", t=NJ), in_=st[("o_sb", n)][:])
+
+        stages = {
+            "load": load, "gate": gate, "qtr": qtr, "qe": qe, "qq": qq, "ctr": ctr, "cTe": cTe, "cTq": cTq,
+            "cg": cg, "cq": cq, "mm1": mm1, "p0": p0, "p1": p1, "p2": p2, "pw": pw, "kk": kk, "ex": ex,
+            "etr": etr, "red": red, "rb": rb, "pj": pj, "pq": pq, "mm2": mm2, "oe": oe, "store": store,
+        }
+        lags = [lag for (name, lag, arg) in SCHEDULE]
+        ctx.enter_context(tc.manual_schedule())
+        for step in range(min(lags), NQ * B + max(lags)):
+            for name, lag, arg in SCHEDULE:
+                n, b = divmod(step - lag, NQ)
+                if n < 0 or n >= B:
+                    continue
+                if arg is None:
+                    stages[name](n, b)
+                elif b == 0:
+                    stages[name](n, arg)

@@ -23,38 +23,13 @@ NG = LS // 512
 NJ = LQ // P
 NQ = 4
 
-SCHEDULE = (
-    ("load", -12, 0),
-    ("mm1", -1, None),
-    ("mm2", 15, 0),
-    ("mm2", 15, 1),
-    ("ctr", -4, None),
-    ("qtr", -5, 0),
-    ("etr", 10, 0),
-    ("kk", 6, 0),
-    ("red", 11, 0),
-    ("cTq", -2, None),
-    ("cq", -3, None),
-    ("rb", 11, 0),
-    ("p0", 0, None),
-    ("p2", 1, None),
-    ("pw", 4, 0),
-    ("ex", 6, None),
-    ("cTe", -3, None),
-    ("qe", -4, 0),
-    ("qe", -3, 1),
-    ("oe", 15, 0),
-    ("oe", 16, 1),
-    ("store", 16, 0),
-    ("cg", -4, None),
-    ("p1", 0, None),
-    ("qq", -2, 0),
-    ("gate", -6, 0),
-    ("pj", 12, 0),
-    ("pj", 13, 1),
-    ("pq", 14, 0),
-    ("pq", 14, 1),
-)
+
+def live(t):
+    return [divmod(t, NQ)] if 0 <= t < NQ * B else []
+
+
+def first(t):
+    return [n for n, b in live(t) if b == 0]
 
 
 def tile_alignment_vector_pa_t_kernel(tc, query, context, matrix, smooth, out):
@@ -63,36 +38,39 @@ def tile_alignment_vector_pa_t_kernel(tc, query, context, matrix, smooth, out):
     with ExitStack() as ctx:
         consts = ctx.enter_context(tc.tile_pool(name="consts", bufs=1))
         sb = ctx.enter_context(tc.tile_pool(name="sb", bufs=2))
-        psum = ctx.enter_context(tc.psum_pool(name="psum", bufs=2))
+        psum = ctx.enter_context(tc.psum_pool(name="psum", bufs=1))
 
         ident_f = consts.tile([P, P], F32, name="ident_f")
         make_identity(nc, ident_f[:])
         ident_b = consts.tile([P, P], BF16, name="ident_b")
         make_identity(nc, ident_b[:])
-        half = consts.tile([P, NT], F32, name="half")
+        half = consts.tile([P, 2], F32, name="half")
         nc.vector.memset(half[:], 0.5)
 
         st = {}
 
-        def load(n, arg):
-            c_sb = sb.tile([P, NG, 4, D], BF16, name="c_sb", bufs=3)
-            nc.sync.dma_start(out=c_sb[:], in_=context[n].rearrange("(g p j) d -> p g j d", g=NG, p=P, j=4))
+        def load(n):
             qr = sb.tile([P, NJ, D], BF16, name="qr", bufs=3)
             nc.sync.dma_start(out=qr[:], in_=query[n].rearrange("(p t) d -> p t d", t=NJ))
             mt = sb.tile([P, NJ, D], BF16, name="mt", bufs=3)
             nc.sync.dma_start(out=mt[:], in_=matrix[n].rearrange("(p t) d -> p t d", t=NJ))
+            c_sb = sb.tile([P, NG, 4, D], BF16, name="c_sb", bufs=3)
+            rows = context[n].rearrange("(g p j) d -> p g j d", g=NG, p=P, j=4)
+            for b in range(NQ):
+                g, h = divmod(b, 2)
+                nc.sync.dma_start(out=c_sb[:, g, 2 * h : 2 * h + 2, :], in_=rows[:, g, 2 * h : 2 * h + 2, :])
             st[("c_sb", n)] = c_sb
             st[("qr", n)] = qr
             st[("mt", n)] = mt
 
-        def gate(n, arg):
+        def gate(n):
             q_sb = sb.tile([P, NJ, D], BF16, name="q_sb")
             nc.vector.tensor_tensor(out=q_sb[:], in0=st[("qr", n)][:], in1=st[("mt", n)][:], op=ALU.mult)
             st[("q_sb", n)] = q_sb
 
-        def qtr(n, arg):
+        def q_transpose(n):
             q_sb = st[("q_sb", n)]
-            qT_ps = psum.tile([P, NJ, 4, P], BF16, name="qT_ps", bufs=1)
+            qT_ps = psum.tile([P, NJ, 4, P], BF16, name="qT_ps")
             for jt in range(NJ):
                 qv = q_sb[:, jt, :].rearrange("p (u w e) -> p u e w", u=2, e=2)
                 for u in range(2):
@@ -101,13 +79,13 @@ def tile_alignment_vector_pa_t_kernel(tc, query, context, matrix, smooth, out):
             st[("qT_ps", n)] = qT_ps
             st[("qg", n)] = sb.tile([P, LQ, 4], BF16, name="qg", align_bytes=64)
 
-        def qe(n, jt):
+        def q_group(n, jt):
             nc.scalar.copy(
-                out=st[("qg", n)][:, P * jt : P * (jt + 1), :],
-                in_=st[("qT_ps", n)][:, jt].rearrange("p t w -> p w t"),
+                out=st[("qg", n)][:, P * jt : P * (jt + 1), :].rearrange("p (c i) t -> p c t i", i=4),
+                in_=st[("qT_ps", n)][:, jt].rearrange("p t (c i) -> p c t i", i=4),
             )
 
-        def qq(n, arg):
+        def q_quantise(n):
             q_codes = sb.tile([P, LQ], U32, name="q_codes", align_bytes=64)
             q_scales = sb.tile([P, LQ], U8, name="q_scales", align_bytes=64)
             nc.vector.quantize_mx(
@@ -115,7 +93,7 @@ def tile_alignment_vector_pa_t_kernel(tc, query, context, matrix, smooth, out):
             )
             st[("q", n)] = (q_codes, q_scales)
 
-        def ctr(n, b):
+        def c_transpose(n, b):
             c32 = st[("c_sb", n)][:].bitcast(F32)
             tr_ps = psum.tile([P, 2, 2, P], F32, name="tr_ps", bufs=2)
             for i2 in range(2):
@@ -124,7 +102,7 @@ def tile_alignment_vector_pa_t_kernel(tc, query, context, matrix, smooth, out):
                     nc.tensor.transpose(tr_ps[:, i2, u, :], c32[:, i // 4, i % 4, P * u : P * (u + 1)], ident_f[:])
             st[("tr_ps", n, b)] = tr_ps
 
-        def cTe(n, b):
+        def cT_group(n, b):
             if b == 0:
                 st[("cTg", n)] = sb.tile([P, LS, 4], BF16, name="cTg", align_bytes=64)
             cTg32 = st[("cTg", n)][:].bitcast(F32)
@@ -133,7 +111,7 @@ def tile_alignment_vector_pa_t_kernel(tc, query, context, matrix, smooth, out):
                 in_=st[("tr_ps", n, b)][:].rearrange("p i u s -> p i s u"),
             )
 
-        def cTq(n, b):
+        def cT_quantise(n, b):
             if b == 0:
                 st[("cT", n)] = (
                     sb.tile([P, LS], U32, name="cT_codes", align_bytes=64),
@@ -147,34 +125,34 @@ def tile_alignment_vector_pa_t_kernel(tc, query, context, matrix, smooth, out):
                 in_=st[("cTg", n)][:, cols, :].rearrange("p s t -> p (s t)"),
             )
 
-        def cg(n, b):
+        def c_group(n, b):
             if b == 0:
                 st[("cg", n)] = sb.tile([P, NG, D, 4], BF16, name="cg", align_bytes=64)
-            g, h = b // 2, b % 2
+            g, h = divmod(b, 2)
             cols = slice(256 * h, 256 * (h + 1))
             nc.vector.tensor_copy(
                 out=st[("cg", n)][:, g, cols, :].rearrange("p (c i) t -> p c t i", i=4),
                 in_=st[("c_sb", n)][:, g, :, cols].rearrange("p t (c i) -> p c t i", i=4),
             )
 
-        def cq(n, b):
+        def c_quantise(n, b):
             if b == 0:
                 st[("c", n)] = (
                     sb.tile([P, NG * D], U32, name="c_codes", align_bytes=64, bufs=6),
                     sb.tile([P, NG * D], U8, name="c_scales", align_bytes=64, bufs=6),
                 )
             c_codes, c_scales = st[("c", n)]
-            g, h = b // 2, b % 2
+            g, h = divmod(b, 2)
             nc.vector.quantize_mx(
                 out=c_codes[:, 256 * b : 256 * (b + 1)].bitcast(FP8X4),
                 scales=c_scales[:, 256 * b : 256 * (b + 1)],
                 in_=st[("cg", n)][:, g, 256 * h : 256 * (h + 1), :].rearrange("p d t -> p (d t)"),
             )
 
-        def mm1(n, b):
+        def scores(n, b):
             q_codes, q_scales = st[("q", n)]
             cT_codes, cT_scales = st[("cT", n)]
-            a_ps = psum.tile([P, 2, LQ], F32, name="a_ps", bufs=2)
+            a_ps = psum.tile([P, 2, LQ], F32, name="a_ps", bufs=3)
             for i2 in range(2):
                 i = 2 * b + i2
                 nc.tensor.matmul_mx(
@@ -188,38 +166,42 @@ def tile_alignment_vector_pa_t_kernel(tc, query, context, matrix, smooth, out):
                 )
             st[("a_ps", n, b)] = a_ps
 
-        def p0(n, b):
+        def leak(n, b):
             if b == 0:
-                st[("lr", n)] = sb.tile([P, NT, LQ], F32, name="lr", bufs=4)
-                st[("ss", n)] = sb.tile([P, NT], F32, name="ss", bufs=3)
+                st[("lr", n)] = sb.tile([P, NT, LQ], F32, name="lr", bufs=3)
             nc.scalar.mul(out=st[("lr", n)][:, 2 * b : 2 * b + 2, :], in_=st[("a_ps", n, b)][:], mul=SLOPE)
 
-        def p1(n, b):
+        def leaky(n, b):
             part = st[("lr", n)][:, 2 * b : 2 * b + 2, :]
             nc.vector.tensor_tensor(out=part, in0=st[("a_ps", n, b)][:], in1=part, op=ALU.max)
 
-        def p2(n, b):
+        def squares(n, b):
+            if b == 0:
+                st[("ss", n)] = sb.tile([P, NT], F32, name="ss", bufs=3)
             for i in (2 * b, 2 * b + 1):
                 junk = sb.tile([P, LQ], BF16, name="junk")
                 nc.scalar.activation(
                     out=junk[:], in_=st[("lr", n)][:, i, :], func=ACT.Square, accum_out=st[("ss", n)][:, i : i + 1]
                 )
 
-        def pw(n, arg):
-            nrm = sb.tile([P, NT], F32, name="nrm", bufs=3)
-            nc.gpsimd.tensor_tensor(out=nrm[:], in0=st[("ss", n)][:], in1=half[:], op=ALU.pow)
-            st[("nrm", n)] = nrm
+        def norm(n, b):
+            if b == 0:
+                st[("nrm", n)] = sb.tile([P, NT], F32, name="nrm", bufs=3)
+                st[("nsc", n)] = sb.tile([P, NT], F32, name="nsc", bufs=3)
+            two = slice(2 * b, 2 * b + 2)
+            nc.gpsimd.tensor_tensor(out=st[("nrm", n)][:, two], in0=st[("ss", n)][:, two], in1=half[:], op=ALU.pow)
+            nc.gpsimd.tensor_scalar(
+                out=st[("nsc", n)][:, two], in0=st[("nrm", n)][:, two],
+                scalar1=EPS, scalar2=1.0 / smooth, op0=ALU.add, op1=ALU.mult,
+            )
 
-        def kk(n, arg):
-            nre = sb.tile([P, NT], F32, name="nre", bufs=3)
-            nc.vector.tensor_scalar(out=nre[:], in0=st[("nrm", n)][:], scalar1=EPS, scalar2=None, op0=ALU.add)
-            rec = sb.tile([P, NT], F32, name="rec", bufs=3)
-            nc.vector.reciprocal(out=rec[:], in_=nre[:])
-            kt = sb.tile([P, NT], F32, name="kt", bufs=3)
-            nc.vector.tensor_scalar(out=kt[:], in0=rec[:], scalar1=smooth, scalar2=None, op0=ALU.mult)
-            st[("kt", n)] = kt
+        def factor(n, b):
+            if b == 0:
+                st[("kt", n)] = sb.tile([P, NT], F32, name="kt", bufs=3)
+            two = slice(2 * b, 2 * b + 2)
+            nc.vector.reciprocal(out=st[("kt", n)][:, two], in_=st[("nsc", n)][:, two])
 
-        def ex(n, b):
+        def exponent(n, b):
             if b == 0:
                 st[("ex", n)] = sb.tile([P, NT, LQ], F32, name="ex")
             for i in (2 * b, 2 * b + 1):
@@ -231,8 +213,8 @@ def tile_alignment_vector_pa_t_kernel(tc, query, context, matrix, smooth, out):
                     bias=-smooth,
                 )
 
-        def etr(n, arg):
-            es_ps = psum.tile([P, 4, P], F32, name="es_ps", bufs=1)
+        def e_transpose(n):
+            es_ps = psum.tile([P, 4, P], F32, name="es_ps")
             for jt in range(NJ):
                 for i in range(NT):
                     nc.tensor.matmul(
@@ -245,14 +227,17 @@ def tile_alignment_vector_pa_t_kernel(tc, query, context, matrix, smooth, out):
                     )
             st[("es", n)] = es_ps
 
-        def red(n, arg):
+        def e_sum(n):
             sm = sb.tile([P, NJ], F32, name="sm", bufs=3)
             nc.vector.tensor_reduce(out=sm[:], in_=st[("es", n)][:, 0:NJ, :], axis=AX.X, op=ALU.add)
+            st[("sm", n)] = sm
+
+        def e_inverse(n):
             rs = sb.tile([P, NJ], F32, name="rs", bufs=3)
-            nc.vector.reciprocal(out=rs[:], in_=sm[:])
+            nc.vector.reciprocal(out=rs[:], in_=st[("sm", n)][:])
             st[("rs", n)] = rs
 
-        def rb(n, arg):
+        def spread(n):
             for jt in range(NJ):
                 nc.tensor.matmul(
                     out=st[("es", n)][:, NJ + jt, :],
@@ -262,18 +247,18 @@ def tile_alignment_vector_pa_t_kernel(tc, query, context, matrix, smooth, out):
                     stop=True,
                 )
 
-        def pj(n, g):
+        def p_group(n, g):
             if g == 0:
                 st[("pg", n)] = sb.tile([P, NG, LQ, 4], BF16, name="pg", align_bytes=64)
-            rbv = st[("es", n)][:, NJ : 2 * NJ, :].rearrange("p t w -> p (t w)").unsqueeze(2).to_broadcast([P, LQ, 4])
+            inv = st[("es", n)][:, NJ : 2 * NJ, :].rearrange("p t (c i) -> p (t c) i", i=4)
             nc.vector.tensor_tensor(
-                out=st[("pg", n)][:, g],
-                in0=st[("ex", n)][:, 4 * g : 4 * (g + 1), :].rearrange("p t j -> p j t"),
-                in1=rbv,
+                out=st[("pg", n)][:, g].rearrange("p (c i) t -> p c t i", i=4),
+                in0=st[("ex", n)][:, 4 * g : 4 * (g + 1), :].rearrange("p t (c i) -> p c t i", i=4),
+                in1=inv.unsqueeze(2).to_broadcast([P, LQ // 4, 4, 4]),
                 op=ALU.mult,
             )
 
-        def pq(n, g):
+        def p_quantise(n, g):
             if g == 0:
                 st[("p", n)] = (
                     sb.tile([P, NG * LQ], U32, name="p_codes", align_bytes=64),
@@ -286,10 +271,10 @@ def tile_alignment_vector_pa_t_kernel(tc, query, context, matrix, smooth, out):
                 in_=st[("pg", n)][:, g].rearrange("p j t -> p (j t)"),
             )
 
-        def mm2(n, jt):
+        def attend(n, jt):
             p_codes, p_scales = st[("p", n)]
             c_codes, c_scales = st[("c", n)]
-            o_ps = psum.tile([P, D], F32, name="o_ps", bufs=2)
+            o_ps = psum.tile([P, D], F32, name="o_ps")
             for g in range(NG):
                 lo = LQ * g + P * jt
                 nc.tensor.matmul_mx(
@@ -303,27 +288,66 @@ def tile_alignment_vector_pa_t_kernel(tc, query, context, matrix, smooth, out):
                 )
             st[("o_ps", n, jt)] = o_ps
 
-        def oe(n, jt):
+        def o_copy(n, jt):
             if jt == 0:
                 st[("o_sb", n)] = sb.tile([P, NJ, D], F32, name="o_sb", bufs=3)
             nc.scalar.copy(out=st[("o_sb", n)][:, jt, :], in_=st[("o_ps", n, jt)][:])
 
-        def store(n, arg):
+        def store(n):
             nc.sync.dma_start(out=out[n].rearrange("(p t) d -> p t d", t=NJ), in_=st[("o_sb", n)][:])
 
-        stages = {
-            "load": load, "gate": gate, "qtr": qtr, "qe": qe, "qq": qq, "ctr": ctr, "cTe": cTe, "cTq": cTq,
-            "cg": cg, "cq": cq, "mm1": mm1, "p0": p0, "p1": p1, "p2": p2, "pw": pw, "kk": kk, "ex": ex,
-            "etr": etr, "red": red, "rb": rb, "pj": pj, "pq": pq, "mm2": mm2, "oe": oe, "store": store,
-        }
-        lags = [lag for (name, lag, arg) in SCHEDULE]
         ctx.enter_context(tc.manual_schedule())
-        for step in range(min(lags), NQ * B + max(lags)):
-            for name, lag, arg in SCHEDULE:
-                n, b = divmod(step - lag, NQ)
-                if n < 0 or n >= B:
-                    continue
-                if arg is None:
-                    stages[name](n, b)
-                elif b == 0:
-                    stages[name](n, arg)
+        for t in range(-8, NQ * B + 22):
+            for n in first(t - 22):
+                store(n)
+            for n, b in live(t - 19):
+                if b % 2 == 0:
+                    o_copy(n, b // 2)
+            for n, b in live(t - 18):
+                if b % 2 == 0:
+                    attend(n, b // 2)
+            for n, b in live(t - 3):
+                scores(n, b)
+            for n, b in live(t - 16):
+                if b < NG:
+                    p_quantise(n, b)
+            for n, b in live(t - 15):
+                if b < NG:
+                    p_group(n, b)
+            for n in first(t - 14):
+                e_sum(n)
+            for n, b in live(t - 8):
+                factor(n, b)
+            for n, b in live(t - 5):
+                leaky(n, b)
+            for n in first(t - 14):
+                e_inverse(n)
+                spread(n)
+            for n in first(t - 13):
+                e_transpose(n)
+            for n, b in live(t - 9):
+                exponent(n, b)
+            for n, b in live(t - 7):
+                norm(n, b)
+            for n, b in live(t - 6):
+                squares(n, b)
+            for n, b in live(t - 4):
+                leak(n, b)
+            for n, b in live(t - 2):
+                cT_quantise(n, b)
+            for n in first(t - 2):
+                q_quantise(n)
+            for n, b in live(t - 1):
+                cT_group(n, b)
+                c_quantise(n, b)
+            for n, b in live(t):
+                if b < NJ:
+                    q_group(n, b)
+                c_transpose(n, b)
+                c_group(n, b)
+            for n in first(t + 1):
+                q_transpose(n)
+            for n in first(t + 2):
+                gate(n)
+            for n in first(t + 8):
+                load(n)

@@ -46,6 +46,8 @@ def tile_alignment_vector_pa_t_kernel(tc, query, context, matrix, smooth, out):
         make_identity(nc, ident_b[:])
         half = consts.tile([P, 2], F32, name="half")
         nc.vector.memset(half[:], 0.5)
+        minus = consts.tile([P, 2], F32, name="minus")
+        nc.vector.memset(minus[:], -1.0)
 
         st = {}
 
@@ -138,8 +140,8 @@ def tile_alignment_vector_pa_t_kernel(tc, query, context, matrix, smooth, out):
         def c_quantise(n, b):
             if b == 0:
                 st[("c", n)] = (
-                    sb.tile([P, NG * D], U32, name="c_codes", align_bytes=64, bufs=6),
-                    sb.tile([P, NG * D], U8, name="c_scales", align_bytes=64, bufs=6),
+                    sb.tile([P, NG * D], U32, name="c_codes", align_bytes=64, bufs=5),
+                    sb.tile([P, NG * D], U8, name="c_scales", align_bytes=64, bufs=5),
                 )
             c_codes, c_scales = st[("c", n)]
             g, h = divmod(b, 2)
@@ -188,18 +190,14 @@ def tile_alignment_vector_pa_t_kernel(tc, query, context, matrix, smooth, out):
             if b == 0:
                 st[("nrm", n)] = sb.tile([P, NT], F32, name="nrm", bufs=3)
                 st[("nsc", n)] = sb.tile([P, NT], F32, name="nsc", bufs=3)
+                st[("kt", n)] = sb.tile([P, NT], F32, name="kt", bufs=3)
             two = slice(2 * b, 2 * b + 2)
             nc.gpsimd.tensor_tensor(out=st[("nrm", n)][:, two], in0=st[("ss", n)][:, two], in1=half[:], op=ALU.pow)
             nc.gpsimd.tensor_scalar(
                 out=st[("nsc", n)][:, two], in0=st[("nrm", n)][:, two],
                 scalar1=EPS, scalar2=1.0 / smooth, op0=ALU.add, op1=ALU.mult,
             )
-
-        def factor(n, b):
-            if b == 0:
-                st[("kt", n)] = sb.tile([P, NT], F32, name="kt", bufs=3)
-            two = slice(2 * b, 2 * b + 2)
-            nc.vector.reciprocal(out=st[("kt", n)][:, two], in_=st[("nsc", n)][:, two])
+            nc.gpsimd.tensor_tensor(out=st[("kt", n)][:, two], in0=st[("nsc", n)][:, two], in1=minus[:], op=ALU.pow)
 
         def exponent(n, b):
             if b == 0:
@@ -293,61 +291,60 @@ def tile_alignment_vector_pa_t_kernel(tc, query, context, matrix, smooth, out):
                 st[("o_sb", n)] = sb.tile([P, NJ, D], F32, name="o_sb", bufs=3)
             nc.scalar.copy(out=st[("o_sb", n)][:, jt, :], in_=st[("o_ps", n, jt)][:])
 
-        def store(n):
-            nc.sync.dma_start(out=out[n].rearrange("(p t) d -> p t d", t=NJ), in_=st[("o_sb", n)][:])
+        def store(n, jt):
+            nc.sync.dma_start(out=out[n].rearrange("(p t) d -> p t d", t=NJ)[:, jt, :], in_=st[("o_sb", n)][:, jt, :])
 
         ctx.enter_context(tc.manual_schedule())
         for t in range(-8, NQ * B + 22):
-            for n in first(t - 22):
-                store(n)
-            for n, b in live(t - 19):
-                if b % 2 == 0:
-                    o_copy(n, b // 2)
-            for n, b in live(t - 18):
-                if b % 2 == 0:
-                    attend(n, b // 2)
+            for n in first(t + 8):
+                load(n)
             for n, b in live(t - 3):
                 scores(n, b)
-            for n, b in live(t - 16):
-                if b < NG:
-                    p_quantise(n, b)
-            for n, b in live(t - 15):
-                if b < NG:
-                    p_group(n, b)
-            for n in first(t - 14):
-                e_sum(n)
-            for n, b in live(t - 8):
-                factor(n, b)
-            for n, b in live(t - 5):
-                leaky(n, b)
-            for n in first(t - 14):
-                e_inverse(n)
-                spread(n)
-            for n in first(t - 13):
-                e_transpose(n)
-            for n, b in live(t - 9):
-                exponent(n, b)
-            for n, b in live(t - 7):
-                norm(n, b)
-            for n, b in live(t - 6):
-                squares(n, b)
-            for n, b in live(t - 4):
-                leak(n, b)
+            for n, b in live(t - 17):
+                if b % 2 == 0:
+                    attend(n, b // 2)
+            for n in first(t + 2):
+                gate(n)
+            for n in first(t + 1):
+                q_transpose(n)
+            for n, b in live(t):
+                c_transpose(n, b)
+                c_group(n, b)
+                if b < NJ:
+                    q_group(n, b)
+            for n, b in live(t - 1):
+                cT_group(n, b)
+                c_quantise(n, b)
             for n, b in live(t - 2):
                 cT_quantise(n, b)
             for n in first(t - 2):
                 q_quantise(n)
-            for n, b in live(t - 1):
-                cT_group(n, b)
-                c_quantise(n, b)
-            for n, b in live(t):
-                if b < NJ:
-                    q_group(n, b)
-                c_transpose(n, b)
-                c_group(n, b)
-            for n in first(t + 1):
-                q_transpose(n)
-            for n in first(t + 2):
-                gate(n)
-            for n in first(t + 8):
-                load(n)
+            for n, b in live(t - 4):
+                leak(n, b)
+            for n in first(t - 13):
+                e_sum(n)
+            for n, b in live(t - 5):
+                leaky(n, b)
+            for n, b in live(t - 6):
+                squares(n, b)
+            for n, b in live(t - 7):
+                norm(n, b)
+            for n, b in live(t - 8):
+                exponent(n, b)
+            for n in first(t - 12):
+                e_transpose(n)
+            for n in first(t - 13):
+                e_inverse(n)
+                spread(n)
+            for n, b in live(t - 14):
+                if b < NG:
+                    p_group(n, b)
+            for n, b in live(t - 15):
+                if b < NG:
+                    p_quantise(n, b)
+            for n, b in live(t - 18):
+                if b % 2 == 0:
+                    o_copy(n, b // 2)
+            for n, b in live(t - 19):
+                if b % 2 == 0:
+                    store(n, b // 2)

@@ -46,8 +46,6 @@ def tile_alignment_vector_pa_t_kernel(tc, query, context, matrix, smooth, out):
         make_identity(nc, ident_b[:])
         half = consts.tile([P, 2], F32, name="half")
         nc.vector.memset(half[:], 0.5)
-        minus = consts.tile([P, 2], F32, name="minus")
-        nc.vector.memset(minus[:], -1.0)
 
         st = {}
 
@@ -140,8 +138,8 @@ def tile_alignment_vector_pa_t_kernel(tc, query, context, matrix, smooth, out):
         def c_quantise(n, b):
             if b == 0:
                 st[("c", n)] = (
-                    sb.tile([P, NG * D], U32, name="c_codes", align_bytes=64, bufs=5),
-                    sb.tile([P, NG * D], U8, name="c_scales", align_bytes=64, bufs=5),
+                    sb.tile([P, NG * D], U32, name="c_codes", align_bytes=64, bufs=6),
+                    sb.tile([P, NG * D], U8, name="c_scales", align_bytes=64, bufs=6),
                 )
             c_codes, c_scales = st[("c", n)]
             g, h = divmod(b, 2)
@@ -190,14 +188,18 @@ def tile_alignment_vector_pa_t_kernel(tc, query, context, matrix, smooth, out):
             if b == 0:
                 st[("nrm", n)] = sb.tile([P, NT], F32, name="nrm", bufs=3)
                 st[("nsc", n)] = sb.tile([P, NT], F32, name="nsc", bufs=3)
-                st[("kt", n)] = sb.tile([P, NT], F32, name="kt", bufs=3)
             two = slice(2 * b, 2 * b + 2)
             nc.gpsimd.tensor_tensor(out=st[("nrm", n)][:, two], in0=st[("ss", n)][:, two], in1=half[:], op=ALU.pow)
             nc.gpsimd.tensor_scalar(
                 out=st[("nsc", n)][:, two], in0=st[("nrm", n)][:, two],
                 scalar1=EPS, scalar2=1.0 / smooth, op0=ALU.add, op1=ALU.mult,
             )
-            nc.gpsimd.tensor_tensor(out=st[("kt", n)][:, two], in0=st[("nsc", n)][:, two], in1=minus[:], op=ALU.pow)
+
+        def factor(n, b):
+            if b == 0:
+                st[("kt", n)] = sb.tile([P, NT], F32, name="kt", bufs=3)
+            two = slice(2 * b, 2 * b + 2)
+            nc.vector.reciprocal(out=st[("kt", n)][:, two], in_=st[("nsc", n)][:, two])
 
         def exponent(n, b):
             if b == 0:
@@ -295,12 +297,12 @@ def tile_alignment_vector_pa_t_kernel(tc, query, context, matrix, smooth, out):
             nc.sync.dma_start(out=out[n].rearrange("(p t) d -> p t d", t=NJ)[:, jt, :], in_=st[("o_sb", n)][:, jt, :])
 
         ctx.enter_context(tc.manual_schedule())
-        for t in range(-8, NQ * B + 22):
+        for t in range(-8, NQ * B + 23):
             for n in first(t + 8):
                 load(n)
             for n, b in live(t - 3):
                 scores(n, b)
-            for n, b in live(t - 17):
+            for n, b in live(t - 18):
                 if b % 2 == 0:
                     attend(n, b // 2)
             for n in first(t + 2):
@@ -321,7 +323,7 @@ def tile_alignment_vector_pa_t_kernel(tc, query, context, matrix, smooth, out):
                 q_quantise(n)
             for n, b in live(t - 4):
                 leak(n, b)
-            for n in first(t - 13):
+            for n in first(t - 14):
                 e_sum(n)
             for n, b in live(t - 5):
                 leaky(n, b)
@@ -330,21 +332,23 @@ def tile_alignment_vector_pa_t_kernel(tc, query, context, matrix, smooth, out):
             for n, b in live(t - 7):
                 norm(n, b)
             for n, b in live(t - 8):
+                factor(n, b)
+            for n, b in live(t - 9):
                 exponent(n, b)
-            for n in first(t - 12):
-                e_transpose(n)
             for n in first(t - 13):
+                e_transpose(n)
+            for n in first(t - 14):
                 e_inverse(n)
                 spread(n)
-            for n, b in live(t - 14):
-                if b < NG:
-                    p_group(n, b)
             for n, b in live(t - 15):
                 if b < NG:
+                    p_group(n, b)
+            for n, b in live(t - 16):
+                if b < NG:
                     p_quantise(n, b)
-            for n, b in live(t - 18):
+            for n, b in live(t - 19):
                 if b % 2 == 0:
                     o_copy(n, b // 2)
-            for n, b in live(t - 19):
+            for n, b in live(t - 20):
                 if b % 2 == 0:
                     store(n, b // 2)

@@ -42,8 +42,6 @@ def tile_alignment_vector_pa_t_kernel(tc, query, context, matrix, smooth, out):
 
         ident_f = consts.tile([P, P], F32, name="ident_f")
         make_identity(nc, ident_f[:])
-        ident_b = consts.tile([P, P], BF16, name="ident_b")
-        make_identity(nc, ident_b[:])
         half = consts.tile([P, 2], F32, name="half")
         nc.vector.memset(half[:], 0.5)
 
@@ -70,19 +68,18 @@ def tile_alignment_vector_pa_t_kernel(tc, query, context, matrix, smooth, out):
 
         def q_transpose(n):
             q_sb = st[("q_sb", n)]
-            qT_ps = psum.tile([P, NJ, 4, P], BF16, name="qT_ps")
+            q32 = q_sb[:].bitcast(F32)
+            qT_ps = psum.tile([P, NJ, 2, P], F32, name="qT_ps")
             for jt in range(NJ):
-                qv = q_sb[:, jt, :].rearrange("p (u w e) -> p u e w", u=2, e=2)
                 for u in range(2):
-                    for e in range(2):
-                        nc.tensor.transpose(qT_ps[:, jt, 2 * u + e, :], qv[:, u, e, :], ident_b[:])
+                    nc.tensor.transpose(qT_ps[:, jt, u, :], q32[:, jt, P * u : P * (u + 1)], ident_f[:])
             st[("qT_ps", n)] = qT_ps
             st[("qg", n)] = sb.tile([P, LQ, 4], BF16, name="qg", align_bytes=64)
 
-        def q_group(n, jt):
+        def q_group(n):
             nc.scalar.copy(
-                out=st[("qg", n)][:, P * jt : P * (jt + 1), :].rearrange("p (c i) t -> p c t i", i=4),
-                in_=st[("qT_ps", n)][:, jt].rearrange("p t (c i) -> p c t i", i=4),
+                out=st[("qg", n)][:].bitcast(F32).rearrange("p (i s) u -> p i s u", i=NJ),
+                in_=st[("qT_ps", n)][:].rearrange("p i u s -> p i s u"),
             )
 
         def q_quantise(n):
@@ -312,8 +309,8 @@ def tile_alignment_vector_pa_t_kernel(tc, query, context, matrix, smooth, out):
             for n, b in live(t):
                 c_transpose(n, b)
                 c_group(n, b)
-                if b < NJ:
-                    q_group(n, b)
+                if b == 1:
+                    q_group(n)
             for n, b in live(t - 1):
                 cT_group(n, b)
                 c_quantise(n, b)

@@ -42,7 +42,7 @@ def tile_alignment_vector_pa_t_kernel(tc, query, context, matrix, smooth, out):
 
         ident_f = consts.tile([P, P], F32, name="ident_f")
         make_identity(nc, ident_f[:])
-        half = consts.tile([P, 2], F32, name="half")
+        half = consts.tile([P, 4], F32, name="half")
         nc.vector.memset(half[:], 0.5)
 
         st = {}
@@ -52,7 +52,7 @@ def tile_alignment_vector_pa_t_kernel(tc, query, context, matrix, smooth, out):
             nc.sync.dma_start(out=qr[:], in_=query[n].rearrange("(p t) d -> p t d", t=NJ))
             mt = sb.tile([P, NJ, D], BF16, name="mt", bufs=3)
             nc.sync.dma_start(out=mt[:], in_=matrix[n].rearrange("(p t) d -> p t d", t=NJ))
-            c_sb = sb.tile([P, NG, 4, D], BF16, name="c_sb", bufs=3)
+            c_sb = sb.tile([P, NG, 4, D], BF16, name="c_sb", bufs=4)
             rows = context[n].rearrange("(g p j) d -> p g j d", g=NG, p=P, j=4)
             for b in range(NQ):
                 g, h = divmod(b, 2)
@@ -83,8 +83,8 @@ def tile_alignment_vector_pa_t_kernel(tc, query, context, matrix, smooth, out):
             )
 
         def q_quantise(n):
-            q_codes = sb.tile([P, LQ], U32, name="q_codes", align_bytes=64)
-            q_scales = sb.tile([P, LQ], U8, name="q_scales", align_bytes=64)
+            q_codes = sb.tile([P, LQ], U32, name="q_codes", align_bytes=64, bufs=3)
+            q_scales = sb.tile([P, LQ], U8, name="q_scales", align_bytes=64, bufs=3)
             nc.vector.quantize_mx(
                 out=q_codes[:].bitcast(FP8X4), scales=q_scales[:], in_=st[("qg", n)][:].rearrange("p j t -> p (j t)")
             )
@@ -108,42 +108,39 @@ def tile_alignment_vector_pa_t_kernel(tc, query, context, matrix, smooth, out):
                 in_=st[("tr_ps", n, b)][:].rearrange("p i u s -> p i s u"),
             )
 
-        def cT_quantise(n, b):
-            if b == 0:
+        def cT_quantise(n, h):
+            if h == 0:
                 st[("cT", n)] = (
                     sb.tile([P, LS], U32, name="cT_codes", align_bytes=64),
                     sb.tile([P, LS], U8, name="cT_scales", align_bytes=64),
                 )
             cT_codes, cT_scales = st[("cT", n)]
-            cols = slice(2 * P * b, 2 * P * (b + 1))
+            cols = slice(512 * h, 512 * (h + 1))
             nc.vector.quantize_mx(
                 out=cT_codes[:, cols].bitcast(FP8X4),
                 scales=cT_scales[:, cols],
                 in_=st[("cTg", n)][:, cols, :].rearrange("p s t -> p (s t)"),
             )
 
-        def c_group(n, b):
-            if b == 0:
+        def c_group(n, g):
+            if g == 0:
                 st[("cg", n)] = sb.tile([P, NG, D, 4], BF16, name="cg", align_bytes=64)
-            g, h = divmod(b, 2)
-            cols = slice(256 * h, 256 * (h + 1))
             nc.vector.tensor_copy(
-                out=st[("cg", n)][:, g, cols, :].rearrange("p (c i) t -> p c t i", i=4),
-                in_=st[("c_sb", n)][:, g, :, cols].rearrange("p t (c i) -> p c t i", i=4),
+                out=st[("cg", n)][:, g].rearrange("p (c i) t -> p c t i", i=4),
+                in_=st[("c_sb", n)][:, g].rearrange("p t (c i) -> p c t i", i=4),
             )
 
-        def c_quantise(n, b):
-            if b == 0:
+        def c_quantise(n, g):
+            if g == 0:
                 st[("c", n)] = (
                     sb.tile([P, NG * D], U32, name="c_codes", align_bytes=64, bufs=6),
                     sb.tile([P, NG * D], U8, name="c_scales", align_bytes=64, bufs=6),
                 )
             c_codes, c_scales = st[("c", n)]
-            g, h = divmod(b, 2)
             nc.vector.quantize_mx(
-                out=c_codes[:, 256 * b : 256 * (b + 1)].bitcast(FP8X4),
-                scales=c_scales[:, 256 * b : 256 * (b + 1)],
-                in_=st[("cg", n)][:, g, 256 * h : 256 * (h + 1), :].rearrange("p d t -> p (d t)"),
+                out=c_codes[:, D * g : D * (g + 1)].bitcast(FP8X4),
+                scales=c_scales[:, D * g : D * (g + 1)],
+                in_=st[("cg", n)][:, g].rearrange("p d t -> p (d t)"),
             )
 
         def scores(n, b):
@@ -181,26 +178,26 @@ def tile_alignment_vector_pa_t_kernel(tc, query, context, matrix, smooth, out):
                     out=junk[:], in_=st[("lr", n)][:, i, :], func=ACT.Square, accum_out=st[("ss", n)][:, i : i + 1]
                 )
 
-        def norm(n, b):
-            if b == 0:
+        def norm(n, h):
+            if h == 0:
                 st[("nrm", n)] = sb.tile([P, NT], F32, name="nrm", bufs=3)
                 st[("nsc", n)] = sb.tile([P, NT], F32, name="nsc", bufs=3)
-            two = slice(2 * b, 2 * b + 2)
-            nc.gpsimd.tensor_tensor(out=st[("nrm", n)][:, two], in0=st[("ss", n)][:, two], in1=half[:], op=ALU.pow)
+            four = slice(4 * h, 4 * h + 4)
+            nc.gpsimd.tensor_tensor(out=st[("nrm", n)][:, four], in0=st[("ss", n)][:, four], in1=half[:], op=ALU.pow)
             nc.gpsimd.tensor_scalar(
-                out=st[("nsc", n)][:, two], in0=st[("nrm", n)][:, two],
+                out=st[("nsc", n)][:, four], in0=st[("nrm", n)][:, four],
                 scalar1=EPS, scalar2=1.0 / smooth, op0=ALU.add, op1=ALU.mult,
             )
 
-        def factor(n, b):
-            if b == 0:
+        def factor(n, h):
+            if h == 0:
                 st[("kt", n)] = sb.tile([P, NT], F32, name="kt", bufs=3)
-            two = slice(2 * b, 2 * b + 2)
-            nc.vector.reciprocal(out=st[("kt", n)][:, two], in_=st[("nsc", n)][:, two])
+            four = slice(4 * h, 4 * h + 4)
+            nc.vector.reciprocal(out=st[("kt", n)][:, four], in_=st[("nsc", n)][:, four])
 
         def exponent(n, b):
             if b == 0:
-                st[("ex", n)] = sb.tile([P, NT, LQ], F32, name="ex")
+                st[("ex", n)] = sb.tile([P, NT, LQ], F32, name="ex", bufs=3)
             for i in (2 * b, 2 * b + 1):
                 nc.scalar.activation(
                     out=st[("ex", n)][:, i, :],
@@ -294,58 +291,65 @@ def tile_alignment_vector_pa_t_kernel(tc, query, context, matrix, smooth, out):
             nc.sync.dma_start(out=out[n].rearrange("(p t) d -> p t d", t=NJ)[:, jt, :], in_=st[("o_sb", n)][:, jt, :])
 
         ctx.enter_context(tc.manual_schedule())
-        for t in range(-8, NQ * B + 23):
+        for t in range(-8, NQ * B + 25):
             for n in first(t + 8):
                 load(n)
-            for n, b in live(t - 3):
+            for n, b in live(t - 4):
                 scores(n, b)
-            for n, b in live(t - 18):
+            for n, b in live(t - 20):
                 if b % 2 == 0:
                     attend(n, b // 2)
-            for n in first(t + 2):
+            for n in first(t + 6):
                 gate(n)
-            for n in first(t + 1):
+            for n in first(t + 5):
                 q_transpose(n)
             for n, b in live(t):
                 c_transpose(n, b)
-                c_group(n, b)
-                if b == 1:
-                    q_group(n)
+            for n, b in live(t - 3):
+                if b < NG:
+                    c_group(n, b)
+            for n in first(t + 4):
+                q_group(n)
             for n, b in live(t - 1):
                 cT_group(n, b)
-                c_quantise(n, b)
-            for n, b in live(t - 2):
-                cT_quantise(n, b)
-            for n in first(t - 2):
-                q_quantise(n)
-            for n, b in live(t - 4):
-                leak(n, b)
-            for n in first(t - 14):
-                e_sum(n)
             for n, b in live(t - 5):
-                leaky(n, b)
+                if b in (0, 3):
+                    c_quantise(n, b // 3)
+            for n, b in live(t - 3):
+                if b % 2 == 0:
+                    cT_quantise(n, b // 2)
+            for n in first(t + 2):
+                q_quantise(n)
+            for n, b in live(t - 5):
+                leak(n, b)
+            for n in first(t - 16):
+                e_sum(n)
             for n, b in live(t - 6):
-                squares(n, b)
+                leaky(n, b)
             for n, b in live(t - 7):
-                norm(n, b)
+                squares(n, b)
             for n, b in live(t - 8):
-                factor(n, b)
+                if b % 2 == 1:
+                    norm(n, b // 2)
             for n, b in live(t - 9):
+                if b % 2 == 1:
+                    factor(n, b // 2)
+            for n, b in live(t - 11):
                 exponent(n, b)
-            for n in first(t - 13):
+            for n in first(t - 15):
                 e_transpose(n)
-            for n in first(t - 14):
+            for n in first(t - 16):
                 e_inverse(n)
                 spread(n)
-            for n, b in live(t - 15):
+            for n, b in live(t - 17):
                 if b < NG:
                     p_group(n, b)
-            for n, b in live(t - 16):
+            for n, b in live(t - 18):
                 if b < NG:
                     p_quantise(n, b)
-            for n, b in live(t - 19):
+            for n, b in live(t - 21):
                 if b % 2 == 0:
                     o_copy(n, b // 2)
-            for n, b in live(t - 20):
+            for n, b in live(t - 22):
                 if b % 2 == 0:
                     store(n, b // 2)

@@ -21,6 +21,7 @@ FLOPS = 2 * 2 * B * LQ * LS * D
 NT = LS // P
 NG = LS // 512
 NJ = LQ // P
+BOTH = (0, 1)
 NQ = 4
 
 
@@ -48,15 +49,16 @@ def tile_alignment_vector_pa_t_kernel(tc, query, context, matrix, smooth, out):
         st = {}
 
         def load(n):
-            qr = sb.tile([P, NJ, D], BF16, name="qr", bufs=3)
-            nc.sync.dma_start(out=qr[:], in_=query[n].rearrange("(p t) d -> p t d", t=NJ))
-            mt = sb.tile([P, NJ, D], BF16, name="mt", bufs=3)
-            nc.sync.dma_start(out=mt[:], in_=matrix[n].rearrange("(p t) d -> p t d", t=NJ))
             c_sb = sb.tile([P, NG, 4, D], BF16, name="c_sb", bufs=4)
             rows = context[n].rearrange("(g p j) d -> p g j d", g=NG, p=P, j=4)
             for b in range(NQ):
                 g, h = divmod(b, 2)
                 nc.sync.dma_start(out=c_sb[:, g, 2 * h : 2 * h + 2, :], in_=rows[:, g, 2 * h : 2 * h + 2, :])
+                if b == 0:
+                    qr = sb.tile([P, NJ, D], BF16, name="qr", bufs=3)
+                    nc.sync.dma_start(out=qr[:], in_=query[n].rearrange("(p t) d -> p t d", t=NJ))
+                    mt = sb.tile([P, NJ, D], BF16, name="mt", bufs=3)
+                    nc.sync.dma_start(out=mt[:], in_=matrix[n].rearrange("(p t) d -> p t d", t=NJ))
             st[("c_sb", n)] = c_sb
             st[("qr", n)] = qr
             st[("mt", n)] = mt
@@ -69,7 +71,7 @@ def tile_alignment_vector_pa_t_kernel(tc, query, context, matrix, smooth, out):
         def q_transpose(n):
             q_sb = st[("q_sb", n)]
             q32 = q_sb[:].bitcast(F32)
-            qT_ps = psum.tile([P, NJ, 2, P], F32, name="qT_ps")
+            qT_ps = psum.tile([P, NJ, 2, P], F32, name="qT_ps", tag="qT_ps")
             for jt in range(NJ):
                 for u in range(2):
                     nc.tensor.transpose(qT_ps[:, jt, u, :], q32[:, jt, P * u : P * (u + 1)], ident_f[:])
@@ -146,7 +148,7 @@ def tile_alignment_vector_pa_t_kernel(tc, query, context, matrix, smooth, out):
         def scores(n, b):
             q_codes, q_scales = st[("q", n)]
             cT_codes, cT_scales = st[("cT", n)]
-            a_ps = psum.tile([P, 2, LQ], F32, name="a_ps", bufs=3)
+            a_ps = psum.tile([P, 2, LQ], F32, name="a_ps", tag="a_ps", bufs=3)
             for i2 in range(2):
                 i = 2 * b + i2
                 nc.tensor.matmul_mx(
@@ -207,68 +209,75 @@ def tile_alignment_vector_pa_t_kernel(tc, query, context, matrix, smooth, out):
                     bias=-smooth,
                 )
 
-        def e_transpose(n):
-            es_ps = psum.tile([P, 4, P], F32, name="es_ps")
-            for jt in range(NJ):
-                for i in range(NT):
+        def e_bank(n, jts):
+            if n < B - 2:
+                es_ps = psum.tile([P, 2, len(jts), P], F32, name="es_ps")
+            else:
+                es_ps = psum.tile([P, 2, len(jts), P], F32, name="es_last", tag="a_ps", bufs=3)
+            st[("es", n, jts)] = es_ps
+
+        def e_transpose(n, jts, tiles):
+            for k, jt in enumerate(jts):
+                for i in tiles:
                     nc.tensor.matmul(
-                        out=es_ps[:, jt, :],
+                        out=st[("es", n, jts)][:, 0, k, :],
                         lhsT=st[("ex", n)][:, i, P * jt : P * (jt + 1)],
                         rhs=ident_f[:],
                         is_transpose=True,
                         start=(i == 0),
                         stop=(i == NT - 1),
                     )
-            st[("es", n)] = es_ps
 
-        def e_sum(n):
-            sm = sb.tile([P, NJ], F32, name="sm", bufs=3)
-            nc.vector.tensor_reduce(out=sm[:], in_=st[("es", n)][:, 0:NJ, :], axis=AX.X, op=ALU.add)
-            st[("sm", n)] = sm
+        def e_sum(n, jts):
+            sm = sb.tile([P, len(jts)], F32, name="sm", bufs=3)
+            nc.vector.tensor_reduce(out=sm[:], in_=st[("es", n, jts)][:, 0], axis=AX.X, op=ALU.add)
+            st[("sm", n, jts)] = sm
 
-        def e_inverse(n):
-            rs = sb.tile([P, NJ], F32, name="rs", bufs=3)
-            nc.vector.reciprocal(out=rs[:], in_=st[("sm", n)][:])
-            st[("rs", n)] = rs
+        def e_inverse(n, jts):
+            rs = sb.tile([P, len(jts)], F32, name="rs", bufs=3)
+            nc.vector.reciprocal(out=rs[:], in_=st[("sm", n, jts)][:])
+            st[("rs", n, jts)] = rs
 
-        def spread(n):
-            for jt in range(NJ):
+        def spread(n, jts):
+            for k in range(len(jts)):
                 nc.tensor.matmul(
-                    out=st[("es", n)][:, NJ + jt, :],
-                    lhsT=st[("rs", n)][:, jt : jt + 1].to_broadcast([P, P]),
+                    out=st[("es", n, jts)][:, 1, k, :],
+                    lhsT=st[("rs", n, jts)][:, k : k + 1].to_broadcast([P, P]),
                     rhs=ident_f[:],
                     start=True,
                     stop=True,
                 )
 
-        def p_group(n, g):
-            if g == 0:
+        def p_group(n, g, jts):
+            if ("pg", n) not in st:
                 st[("pg", n)] = sb.tile([P, NG, LQ, 4], BF16, name="pg", align_bytes=64)
-            inv = st[("es", n)][:, NJ : 2 * NJ, :].rearrange("p t (c i) -> p (t c) i", i=4)
+            cols = slice(P * jts[0], P * (jts[-1] + 1))
+            inv = st[("es", n, jts)][:, 1].rearrange("p t (c i) -> p (t c) i", i=4)
             nc.vector.tensor_tensor(
-                out=st[("pg", n)][:, g].rearrange("p (c i) t -> p c t i", i=4),
-                in0=st[("ex", n)][:, 4 * g : 4 * (g + 1), :].rearrange("p t (c i) -> p c t i", i=4),
-                in1=inv.unsqueeze(2).to_broadcast([P, LQ // 4, 4, 4]),
+                out=st[("pg", n)][:, g, cols].rearrange("p (c i) t -> p c t i", i=4),
+                in0=st[("ex", n)][:, 4 * g : 4 * (g + 1), cols].rearrange("p t (c i) -> p c t i", i=4),
+                in1=inv.unsqueeze(2).to_broadcast([P, len(jts) * P // 4, 4, 4]),
                 op=ALU.mult,
             )
 
-        def p_quantise(n, g):
-            if g == 0:
+        def p_quantise(n, g, jts):
+            if ("p", n) not in st:
                 st[("p", n)] = (
                     sb.tile([P, NG * LQ], U32, name="p_codes", align_bytes=64),
                     sb.tile([P, NG * LQ], U8, name="p_scales", align_bytes=64),
                 )
             p_codes, p_scales = st[("p", n)]
+            lo, hi = P * jts[0], P * (jts[-1] + 1)
             nc.vector.quantize_mx(
-                out=p_codes[:, LQ * g : LQ * (g + 1)].bitcast(FP8X4),
-                scales=p_scales[:, LQ * g : LQ * (g + 1)],
-                in_=st[("pg", n)][:, g].rearrange("p j t -> p (j t)"),
+                out=p_codes[:, LQ * g + lo : LQ * g + hi].bitcast(FP8X4),
+                scales=p_scales[:, LQ * g + lo : LQ * g + hi],
+                in_=st[("pg", n)][:, g, lo:hi].rearrange("p j t -> p (j t)"),
             )
 
         def attend(n, jt):
             p_codes, p_scales = st[("p", n)]
             c_codes, c_scales = st[("c", n)]
-            o_ps = psum.tile([P, D], F32, name="o_ps")
+            o_ps = psum.tile([P, D], F32, name="o_ps", tag="qT_ps" if (n, jt) == (B - 1, 0) else "o_ps")
             for g in range(NG):
                 lo = LQ * g + P * jt
                 nc.tensor.matmul_mx(
@@ -290,6 +299,7 @@ def tile_alignment_vector_pa_t_kernel(tc, query, context, matrix, smooth, out):
         def store(n, jt):
             nc.sync.dma_start(out=out[n].rearrange("(p t) d -> p t d", t=NJ)[:, jt, :], in_=st[("o_sb", n)][:, jt, :])
 
+        last = B - 1
         ctx.enter_context(tc.manual_schedule())
         for t in range(-8, NQ * B + 25):
             for n in first(t + 8):
@@ -299,31 +309,30 @@ def tile_alignment_vector_pa_t_kernel(tc, query, context, matrix, smooth, out):
             for n, b in live(t - 20):
                 if b % 2 == 0:
                     attend(n, b // 2)
-            for n in first(t + 6):
-                gate(n)
-            for n in first(t + 5):
-                q_transpose(n)
             for n, b in live(t):
                 c_transpose(n, b)
+            for n in first(t):
+                q_transpose(n)
+            for n, b in live(t - 1):
+                cT_group(n, b)
+            for n in first(t - 1):
+                q_group(n)
             for n, b in live(t - 3):
                 if b < NG:
                     c_group(n, b)
-            for n in first(t + 4):
-                q_group(n)
-            for n, b in live(t - 1):
-                cT_group(n, b)
             for n, b in live(t - 5):
                 if b in (0, 3):
                     c_quantise(n, b // 3)
             for n, b in live(t - 3):
                 if b % 2 == 0:
                     cT_quantise(n, b // 2)
-            for n in first(t + 2):
+            for n in first(t - 2):
                 q_quantise(n)
             for n, b in live(t - 5):
                 leak(n, b)
             for n in first(t - 16):
-                e_sum(n)
+                if n < last:
+                    e_sum(n, BOTH)
             for n, b in live(t - 6):
                 leaky(n, b)
             for n, b in live(t - 7):
@@ -337,16 +346,37 @@ def tile_alignment_vector_pa_t_kernel(tc, query, context, matrix, smooth, out):
             for n, b in live(t - 11):
                 exponent(n, b)
             for n in first(t - 15):
-                e_transpose(n)
+                if n < last:
+                    e_bank(n, BOTH)
+                    e_transpose(n, BOTH, range(NT))
             for n in first(t - 16):
-                e_inverse(n)
-                spread(n)
+                if n < last:
+                    e_inverse(n, BOTH)
+                    spread(n, BOTH)
             for n, b in live(t - 17):
-                if b < NG:
-                    p_group(n, b)
+                if b < NG and n < last:
+                    p_group(n, b, BOTH)
             for n, b in live(t - 18):
-                if b < NG:
-                    p_quantise(n, b)
+                if b < NG and n < last:
+                    p_quantise(n, b, BOTH)
+            for n in first(t + 1):
+                gate(n)
+            for n, b in live(t - 12):
+                if n == last:
+                    for jt in BOTH:
+                        if b == 0:
+                            e_bank(n, (jt,))
+                        e_transpose(n, (jt,), range(2 * b, 2 * b + 2))
+            for n in first(t - 16):
+                if n == last:
+                    for stage in (e_sum, e_inverse, spread):
+                        for jt in BOTH:
+                            stage(n, (jt,))
+                    for jt in BOTH:
+                        for g in range(NG):
+                            p_group(n, g, (jt,))
+                        for g in range(NG):
+                            p_quantise(n, g, (jt,))
             for n, b in live(t - 21):
                 if b % 2 == 0:
                     o_copy(n, b // 2)

from contextlib import ExitStack

import concourse.mybir as mybir
from concourse.masks import make_identity

F32 = mybir.dt.float32
BF16 = mybir.dt.bfloat16
U32 = mybir.dt.uint32
U8 = mybir.dt.uint8
FP8X4 = mybir.dt.float8_e4m3fn_x4
ALU = mybir.AluOpType
ACT = mybir.ActivationFunctionType
AX = mybir.AxisListType

B, LQ, LS, D = 16, 256, 1024, 512
P = 128
EPS = 1e-08
SLOPE = 0.1
FLOPS = 2 * 2 * B * LQ * LS * D

NT = LS // P
NG = LS // 512
NJ = LQ // P
BOTH = (0, 1)
NQ = 4


def live(t):
    return [divmod(t, NQ)] if 0 <= t < NQ * B else []


def first(t):
    return [n for n, b in live(t) if b == 0]


def tile_alignment_vector_pa_t_kernel(tc, query, context, matrix, smooth, out):
    nc = tc.nc
    smooth = float(smooth)
    with ExitStack() as ctx:
        consts = ctx.enter_context(tc.tile_pool(name="consts", bufs=1))
        sb = ctx.enter_context(tc.tile_pool(name="sb", bufs=2))
        psum = ctx.enter_context(tc.psum_pool(name="psum", bufs=1))

        ident_f = consts.tile([P, P], F32, name="ident_f")
        make_identity(nc, ident_f[:])
        half = consts.tile([P, 4], F32, name="half")
        nc.vector.memset(half[:], 0.5)

        st = {}

        def load(n):
            c_sb = sb.tile([P, NG, 4, D], BF16, name="c_sb", bufs=4)
            rows = context[n].rearrange("(g p j) d -> p g j d", g=NG, p=P, j=4)
            for b in range(NQ):
                g, h = divmod(b, 2)
                nc.sync.dma_start(out=c_sb[:, g, 2 * h : 2 * h + 2, :], in_=rows[:, g, 2 * h : 2 * h + 2, :])
                if b == 0:
                    qr = sb.tile([P, NJ, D], BF16, name="qr", bufs=3)
                    nc.sync.dma_start(out=qr[:], in_=query[n].rearrange("(p t) d -> p t d", t=NJ))
                    mt = sb.tile([P, NJ, D], BF16, name="mt", bufs=3)
                    nc.sync.dma_start(out=mt[:], in_=matrix[n].rearrange("(p t) d -> p t d", t=NJ))
            st[("c_sb", n)] = c_sb
            st[("qr", n)] = qr
            st[("mt", n)] = mt

        def gate(n):
            q_sb = sb.tile([P, NJ, D], BF16, name="q_sb")
            nc.vector.tensor_tensor(out=q_sb[:], in0=st[("qr", n)][:], in1=st[("mt", n)][:], op=ALU.mult)
            st[("q_sb", n)] = q_sb

        def q_transpose(n):
            q_sb = st[("q_sb", n)]
            q32 = q_sb[:].bitcast(F32)
            qT_ps = psum.tile([P, NJ, 2, P], F32, name="qT_ps", tag="qT_ps")
            for jt in range(NJ):
                for u in range(2):
                    nc.tensor.transpose(qT_ps[:, jt, u, :], q32[:, jt, P * u : P * (u + 1)], ident_f[:])
            st[("qT_ps", n)] = qT_ps
            st[("qg", n)] = sb.tile([P, LQ, 4], BF16, name="qg", align_bytes=64)

        def q_group(n):
            nc.scalar.copy(
                out=st[("qg", n)][:].bitcast(F32).rearrange("p (i s) u -> p i s u", i=NJ),
                in_=st[("qT_ps", n)][:].rearrange("p i u s -> p i s u"),
            )

        def q_quantise(n):
            q_codes = sb.tile([P, LQ], U32, name="q_codes", align_bytes=64, bufs=3)
            q_scales = sb.tile([P, LQ], U8, name="q_scales", align_bytes=64, bufs=3)
            nc.vector.quantize_mx(
                out=q_codes[:].bitcast(FP8X4), scales=q_scales[:], in_=st[("qg", n)][:].rearrange("p j t -> p (j t)")
            )
            st[("q", n)] = (q_codes, q_scales)

        def c_transpose(n, b):
            c32 = st[("c_sb", n)][:].bitcast(F32)
            tr_ps = psum.tile([P, 2, 2, P], F32, name="tr_ps", bufs=2)
            for i2 in range(2):
                i = 2 * b + i2
                for u in range(2):
                    nc.tensor.transpose(tr_ps[:, i2, u, :], c32[:, i // 4, i % 4, P * u : P * (u + 1)], ident_f[:])
            st[("tr_ps", n, b)] = tr_ps

        def cT_group(n, b):
            if b == 0:
                st[("cTg", n)] = sb.tile([P, LS, 4], BF16, name="cTg", align_bytes=64)
            cTg32 = st[("cTg", n)][:].bitcast(F32)
            nc.scalar.copy(
                out=cTg32[:, 2 * P * b : 2 * P * (b + 1), :].rearrange("p (i s) u -> p i s u", i=2),
                in_=st[("tr_ps", n, b)][:].rearrange("p i u s -> p i s u"),
            )

        def cT_quantise(n, h):
            if h == 0:
                st[("cT", n)] = (
                    sb.tile([P, LS], U32, name="cT_codes", align_bytes=64),
                    sb.tile([P, LS], U8, name="cT_scales", align_bytes=64),
                )
            cT_codes, cT_scales = st[("cT", n)]
            cols = slice(512 * h, 512 * (h + 1))
            nc.vector.quantize_mx(
                out=cT_codes[:, cols].bitcast(FP8X4),
                scales=cT_scales[:, cols],
                in_=st[("cTg", n)][:, cols, :].rearrange("p s t -> p (s t)"),
            )

        def c_group(n, g):
            if g == 0:
                st[("cg", n)] = sb.tile([P, NG, D, 4], BF16, name="cg", align_bytes=64)
            nc.vector.tensor_copy(
                out=st[("cg", n)][:, g].rearrange("p (c i) t -> p c t i", i=4),
                in_=st[("c_sb", n)][:, g].rearrange("p t (c i) -> p c t i", i=4),
            )

        def c_quantise(n, g):
            if g == 0:
                st[("c", n)] = (
                    sb.tile([P, NG * D], U32, name="c_codes", align_bytes=64, bufs=6),
                    sb.tile([P, NG * D], U8, name="c_scales", align_bytes=64, bufs=6),
                )
            c_codes, c_scales = st[("c", n)]
            nc.vector.quantize_mx(
                out=c_codes[:, D * g : D * (g + 1)].bitcast(FP8X4),
                scales=c_scales[:, D * g : D * (g + 1)],
                in_=st[("cg", n)][:, g].rearrange("p d t -> p (d t)"),
            )

        def scores(n, b):
            q_codes, q_scales = st[("q", n)]
            cT_codes, cT_scales = st[("cT", n)]
            a_ps = psum.tile([P, 2, LQ], F32, name="a_ps", tag="a_ps", bufs=3)
            for i2 in range(2):
                i = 2 * b + i2
                nc.tensor.matmul_mx(
                    out=a_ps[:, i2, :],
                    lhsT=cT_codes[:, P * i : P * (i + 1)].bitcast(FP8X4),
                    lhsT_scale=cT_scales[:, P * i : P * (i + 1)],
                    rhs=q_codes[:].bitcast(FP8X4),
                    rhs_scale=q_scales[:],
                    start=True,
                    stop=True,
                )
            st[("a_ps", n, b)] = a_ps

        def leak(n, b):
            if b == 0:
                st[("lr", n)] = sb.tile([P, NT, LQ], F32, name="lr", bufs=3)
            nc.scalar.mul(out=st[("lr", n)][:, 2 * b : 2 * b + 2, :], in_=st[("a_ps", n, b)][:], mul=SLOPE)

        def leaky(n, b):
            part = st[("lr", n)][:, 2 * b : 2 * b + 2, :]
            nc.vector.tensor_tensor(out=part, in0=st[("a_ps", n, b)][:], in1=part, op=ALU.max)

        def squares(n, b):
            if b == 0:
                st[("ss", n)] = sb.tile([P, NT], F32, name="ss", bufs=3)
            for i in (2 * b, 2 * b + 1):
                junk = sb.tile([P, LQ], BF16, name="junk")
                nc.scalar.activation(
                    out=junk[:], in_=st[("lr", n)][:, i, :], func=ACT.Square, accum_out=st[("ss", n)][:, i : i + 1]
                )

        def norm(n, h):
            if h == 0:
                st[("nrm", n)] = sb.tile([P, NT], F32, name="nrm", bufs=3)
                st[("nsc", n)] = sb.tile([P, NT], F32, name="nsc", bufs=3)
            four = slice(4 * h, 4 * h + 4)
            nc.gpsimd.tensor_tensor(out=st[("nrm", n)][:, four], in0=st[("ss", n)][:, four], in1=half[:], op=ALU.pow)
            nc.gpsimd.tensor_scalar(
                out=st[("nsc", n)][:, four], in0=st[("nrm", n)][:, four],
                scalar1=EPS, scalar2=1.0 / smooth, op0=ALU.add, op1=ALU.mult,
            )

        def factor(n, h):
            if h == 0:
                st[("kt", n)] = sb.tile([P, NT], F32, name="kt", bufs=3)
            four = slice(4 * h, 4 * h + 4)
            nc.vector.reciprocal(out=st[("kt", n)][:, four], in_=st[("nsc", n)][:, four])

        def exponent(n, b):
            if b == 0:
                st[("ex", n)] = sb.tile([P, NT, LQ], F32, name="ex", bufs=3)
            for i in (2 * b, 2 * b + 1):
                nc.scalar.activation(
                    out=st[("ex", n)][:, i, :],
                    in_=st[("lr", n)][:, i, :],
                    func=ACT.Exp,
                    scale=st[("kt", n)][:, i : i + 1],
                    bias=-smooth,
                )

        def e_bank(n, jts):
            if n < B - 2:
                es_ps = psum.tile([P, 2, len(jts), P], F32, name="es_ps")
            else:
                es_ps = psum.tile([P, 2, len(jts), P], F32, name="es_last", tag="a_ps", bufs=3)
            st[("es", n, jts)] = es_ps

        def e_transpose(n, jts, tiles):
            for k, jt in enumerate(jts):
                for i in tiles:
                    nc.tensor.matmul(
                        out=st[("es", n, jts)][:, 0, k, :],
                        lhsT=st[("ex", n)][:, i, P * jt : P * (jt + 1)],
                        rhs=ident_f[:],
                        is_transpose=True,
                        start=(i == 0),
                        stop=(i == NT - 1),
                    )

        def e_sum(n, jts):
            sm = sb.tile([P, len(jts)], F32, name="sm", bufs=3)
            nc.vector.tensor_reduce(out=sm[:], in_=st[("es", n, jts)][:, 0], axis=AX.X, op=ALU.add)
            st[("sm", n, jts)] = sm

        def e_inverse(n, jts):
            rs = sb.tile([P, len(jts)], F32, name="rs", bufs=3)
            nc.vector.reciprocal(out=rs[:], in_=st[("sm", n, jts)][:])
            st[("rs", n, jts)] = rs

        def spread(n, jts):
            for k in range(len(jts)):
                nc.tensor.matmul(
                    out=st[("es", n, jts)][:, 1, k, :],
                    lhsT=st[("rs", n, jts)][:, k : k + 1].to_broadcast([P, P]),
                    rhs=ident_f[:],
                    start=True,
                    stop=True,
                )

        def p_group(n, g, jts):
            if ("pg", n) not in st:
                st[("pg", n)] = sb.tile([P, NG, LQ, 4], BF16, name="pg", align_bytes=64)
            cols = slice(P * jts[0], P * (jts[-1] + 1))
            inv = st[("es", n, jts)][:, 1].rearrange("p t (c i) -> p (t c) i", i=4)
            nc.vector.tensor_tensor(
                out=st[("pg", n)][:, g, cols].rearrange("p (c i) t -> p c t i", i=4),
                in0=st[("ex", n)][:, 4 * g : 4 * (g + 1), cols].rearrange("p t (c i) -> p c t i", i=4),
                in1=inv.unsqueeze(2).to_broadcast([P, len(jts) * P // 4, 4, 4]),
                op=ALU.mult,
            )

        def p_quantise(n, g, jts):
            if ("p", n) not in st:
                st[("p", n)] = (
                    sb.tile([P, NG * LQ], U32, name="p_codes", align_bytes=64),
                    sb.tile([P, NG * LQ], U8, name="p_scales", align_bytes=64),
                )
            p_codes, p_scales = st[("p", n)]
            lo, hi = P * jts[0], P * (jts[-1] + 1)
            nc.vector.quantize_mx(
                out=p_codes[:, LQ * g + lo : LQ * g + hi].bitcast(FP8X4),
                scales=p_scales[:, LQ * g + lo : LQ * g + hi],
                in_=st[("pg", n)][:, g, lo:hi].rearrange("p j t -> p (j t)"),
            )

        def attend(n, jt):
            p_codes, p_scales = st[("p", n)]
            c_codes, c_scales = st[("c", n)]
            o_ps = psum.tile([P, D], F32, name="o_ps", tag="qT_ps" if (n, jt) == (B - 1, 0) else "o_ps")
            for g in range(NG):
                lo = LQ * g + P * jt
                nc.tensor.matmul_mx(
                    out=o_ps[:],
                    lhsT=p_codes[:, lo : lo + P].bitcast(FP8X4),
                    lhsT_scale=p_scales[:, lo : lo + P],
                    rhs=c_codes[:, D * g : D * (g + 1)].bitcast(FP8X4),
                    rhs_scale=c_scales[:, D * g : D * (g + 1)],
                    start=(g == 0),
                    stop=(g == NG - 1),
                )
            st[("o_ps", n, jt)] = o_ps

        def o_copy(n, jt):
            if jt == 0:
                st[("o_sb", n)] = sb.tile([P, NJ, D], F32, name="o_sb", bufs=3)
            nc.scalar.copy(out=st[("o_sb", n)][:, jt, :], in_=st[("o_ps", n, jt)][:])

        def store(n, jt):
            nc.sync.dma_start(out=out[n].rearrange("(p t) d -> p t d", t=NJ)[:, jt, :], in_=st[("o_sb", n)][:, jt, :])

        last = B - 1
        ctx.enter_context(tc.manual_schedule())
        for t in range(-8, NQ * B + 25):
            for n in first(t + 8):
                load(n)
            for n, b in live(t - 4):
                scores(n, b)
            for n, b in live(t - 20):
                if b % 2 == 0:
                    attend(n, b // 2)
            for n, b in live(t):
                c_transpose(n, b)
            for n in first(t):
                q_transpose(n)
            for n, b in live(t - 1):
                cT_group(n, b)
            for n in first(t - 1):
                q_group(n)
            for n, b in live(t - 3):
                if b < NG:
                    c_group(n, b)
            for n, b in live(t - 5):
                if b in (0, 3):
                    c_quantise(n, b // 3)
            for n, b in live(t - 3):
                if b % 2 == 0:
                    cT_quantise(n, b // 2)
            for n in first(t - 2):
                q_quantise(n)
            for n, b in live(t - 5):
                leak(n, b)
            for n in first(t - 16):
                if n < last:
                    e_sum(n, BOTH)
            for n, b in live(t - 6):
                leaky(n, b)
            for n, b in live(t - 7):
                squares(n, b)
            for n, b in live(t - 8):
                if b % 2 == 1:
                    norm(n, b // 2)
            for n, b in live(t - 9):
                if b % 2 == 1:
                    factor(n, b // 2)
            for n, b in live(t - 11):
                exponent(n, b)
            for n in first(t - 15):
                if n < last:
                    e_bank(n, BOTH)
                    e_transpose(n, BOTH, range(NT))
            for n in first(t - 16):
                if n < last:
                    e_inverse(n, BOTH)
                    spread(n, BOTH)
            for n, b in live(t - 17):
                if b < NG and n < last:
                    p_group(n, b, BOTH)
            for n, b in live(t - 18):
                if b < NG and n < last:
                    p_quantise(n, b, BOTH)
            for n in first(t + 1):
                gate(n)
            for n, b in live(t - 12):
                if n == last:
                    for jt in BOTH:
                        if b == 0:
                            e_bank(n, (jt,))
                        e_transpose(n, (jt,), range(2 * b, 2 * b + 2))
            for n in first(t - 16):
                if n == last:
                    for stage in (e_sum, e_inverse, spread):
                        for jt in BOTH:
                            stage(n, (jt,))
                    for jt in BOTH:
                        for g in range(NG):
                            p_group(n, g, (jt,))
                        for g in range(NG):
                            p_quantise(n, g, (jt,))
            for n, b in live(t - 21):
                if b % 2 == 0:
                    o_copy(n, b // 2)
            for n, b in live(t - 22):
                if b % 2 == 0:
                    store(n, b // 2)
